import numpy as np
import ml_dtypes


def mxq(x, axis, fmt="e4m3"):
    dtype, down = {"e4m3": (ml_dtypes.float8_e4m3fn, 7), "e5m2": (ml_dtypes.float8_e5m2, 14)}[fmt]
    v = np.moveaxis(np.asarray(x, np.float32).astype(ml_dtypes.bfloat16).astype(np.float64), axis, -1)
    blocks = v.reshape(v.shape[:-1] + (-1, 32))
    amax = np.abs(blocks).max(-1, keepdims=True)
    byte = np.maximum(np.where(amax > 0, np.frexp(amax)[1] - 1 + 127, 0) - down, 1)
    scale = np.exp2(byte - 127.0)
    codes = (blocks / scale).astype(np.float32).astype(dtype).astype(np.float64)
    return np.moveaxis((codes * scale).reshape(v.shape), -1, axis)


WIDE = False


def mx_kscale(k):
    if not WIDE:
        return np.ones(k)
    levels = np.array([10, -10, 5, -5, 0])
    a = np.random.permutation(np.resize(levels, k // 512 * 4)).reshape(k // 512, 4)
    idx = np.arange(k)
    return np.exp2(a[idx // 512, idx % 128 // 32])


BF16 = ml_dtypes.bfloat16


def bf(x):
    return np.asarray(x, np.float32).astype(BF16)


def f64(x):
    return np.asarray(x).astype(np.float64)


N, B, C, E, D, R = 4096, 2048, 512, 256, 256, 8
SPREAD = 2.0


def spread(z, lat):
    return (z[:, :, None] * lat[None, :, :]).sum(1)


def setup_inputs():
    s = mx_kscale(C)
    lat = np.random.standard_normal((R, E)) * SPREAD
    return {
        "source": bf(np.random.standard_normal((N, C)) * s),
        "target": bf(spread(np.random.standard_normal((B, R)), lat)),
        "k_right": bf(spread(np.random.standard_normal((N, R)), lat)),
        "WF_right": bf(np.random.standard_normal((D, C)) * 3.0 / np.sqrt(C) / s),
    }


def reference(source, target, k_right, WF_right):
    t, k = f64(target), f64(k_right)
    f = mxq(f64(source), 1, "e4m3") @ mxq(f64(WF_right).T, 0, "e4m3")
    d2 = (t * t).sum(-1, keepdims=True) + (k * k).sum(-1)[None, :] - 2.0 * (f64(target) @ f64(k_right).T)
    dist = np.sqrt(np.maximum(d2, 0.0))
    l = -dist * E ** (-0.5)
    e = np.exp(l - l.max(-1, keepdims=True))
    return (mxq(e, 1, "e4m3") @ mxq(f, 0, "e4m3")) / e.sum(-1, keepdims=True)

@@ -1,0 +1,455 @@
+from contextlib import ExitStack
+
+import concourse.mybir as mybir
+from concourse.masks import make_identity
+
+F32 = mybir.dt.float32
+BF16 = mybir.dt.bfloat16
+U32 = mybir.dt.uint32
+U8 = mybir.dt.uint8
+FP8X4 = mybir.dt.float8_e4m3fn_x4
+ALU = mybir.AluOpType
+ACTF = mybir.ActivationFunctionType
+AX = mybir.AxisListType
+
+P = 128
+N, B, C, E, D = 4096, 2048, 512, 256, 256
+NT = N // P
+BT = B // P
+NCH = N // 512
+FLOPS = 2 * (N * C * D + 2 * B * N * E)
+
+ZR_BUFS = 6
+E_BUFS = 4
+S_BANKS = 4
+X_BANKS = 3
+AHEAD = 2
+PHASE = 4
+
+
+def tile_kanadjunction_pa_kernel(tc, source, target, k_right, WF_right, out):
+    nc = tc.nc
+    with ExitStack() as ctx:
+        keep = ctx.enter_context(tc.tile_pool(name="keep", bufs=1))
+        work = ctx.enter_context(tc.tile_pool(name="work", bufs=1))
+        psum = ctx.enter_context(tc.psum_pool(name="psum", bufs=1))
+        ctx.enter_context(tc.manual_schedule())
+
+        ident_b = keep.tile([P, P], BF16, name="ident_b")
+        make_identity(nc, ident_b[:])
+        ident_f = keep.tile([P, P], F32, name="ident_f")
+        make_identity(nc, ident_f[:])
+        one = keep.tile([P, 1], F32, name="one")
+        nc.vector.memset(one[:], 1.0)
+        warm = keep.tile([P, 1], F32, name="warm")
+        nc.scalar.activation(out=warm[:], in_=one[:], func=ACTF.Sqrt)
+
+        kT = keep.tile([P, 2, N], BF16, name="kT")
+        tT = keep.tile([P, 2, B], BF16, name="tT")
+        kk = keep.tile([P, NT], F32, name="kk")
+        tt = keep.tile([P, BT], F32, name="tt")
+        negtt = keep.tile([P, BT], F32, name="negtt")
+        tt256 = keep.tile([P, BT], F32, name="tt256")
+        zmin = keep.tile([P, BT], F32, name="zmin")
+        bexp = keep.tile([P, BT], F32, name="bexp")
+        rsum = keep.tile([P, BT], F32, name="rsum")
+        rinv = keep.tile([P, BT], F32, name="rinv")
+        junk = keep.tile([P, E], BF16, name="junk")
+        fcodes = keep.tile([P, NCH, D], U32, name="fcodes", align_bytes=64)
+        fscales = keep.tile([P, NCH, D], U8, name="fscales", align_bytes=64)
+        wcodes = keep.tile([P, D], U32, name="wcodes", align_bytes=64)
+        wscales = keep.tile([P, D], U8, name="wscales", align_bytes=64)
+        wf_nat = keep.tile([P, 2, C], BF16, name="wf_nat")
+        wgrp = keep.tile([P, D, 4], BF16, name="wgrp", align_bytes=64)
+
+        k_view = k_right.rearrange("(m p) j -> p m j", p=P)
+        t_view = target.rearrange("(i p) j -> p i j", p=P)
+        s_view = source.rearrange("(a p e) c -> p a (e c)", p=P, e=2)
+        k_nat = [
+            work.tile([P, NT // 2, E], BF16, tag="e", bufs=E_BUFS, name="k_nat%d" % h)
+            for h in range(2)
+        ]
+        t_nat = work.tile([P, BT, E], BF16, tag="e", bufs=E_BUFS, name="t_nat")
+
+        def load_k(q):
+            nc.sync.dma_start(
+                out=k_nat[q // 2][:, 8 * (q % 2) : 8 * (q % 2) + 8, :],
+                in_=k_view[:, 8 * q : 8 * q + 8, :],
+            )
+
+        load_k(0)
+        nc.sync.dma_start(out=t_nat[:, 0:4, :], in_=t_view[:, 0:4, :])
+        load_k(1)
+        load_k(2)
+        load_k(3)
+        nc.sync.dma_start(out=t_nat[:, 4:BT, :], in_=t_view[:, 4:BT, :])
+        nc.sync.dma_start(out=wf_nat[:], in_=WF_right.rearrange("(h p) c -> p h c", p=P))
+
+        src = {}
+
+        def load_src(g):
+            src[g] = work.tile([P, 4, C], BF16, tag="src", bufs=2, name="src")
+            nc.sync.dma_start(
+                out=src[g][:].rearrange("p (u e) c -> p u (e c)", u=2),
+                in_=s_view[:, 2 * g : 2 * g + 2, :],
+            )
+
+        load_src(0)
+        load_src(1)
+
+        def k_tile(m):
+            return k_nat[m // 16][:, m % 16, :]
+
+        def square_t(i):
+            nc.scalar.activation(
+                out=junk[:], in_=t_nat[:, i, :], func=ACTF.Square, accum_out=tt[:, i : i + 1]
+            )
+
+        def square_k(m):
+            nc.scalar.activation(
+                out=junk[:], in_=k_tile(m), func=ACTF.Square, accum_out=kk[:, m : m + 1]
+            )
+
+        def norms_t(a, b):
+            nc.vector.tensor_scalar(
+                out=negtt[:, a:b], in0=tt[:, a:b], scalar1=-1.0, scalar2=None, op0=ALU.mult
+            )
+            nc.vector.tensor_scalar(
+                out=tt256[:, a:b], in0=tt[:, a:b], scalar1=1.0 / 256.0, scalar2=None, op0=ALU.mult
+            )
+
+        bank = {}
+
+        def k_transposes(c):
+            pk = psum.tile([P, 2, 4, P], BF16, tag="x", bufs=X_BANKS, name="pk")
+            bank["k", c] = pk
+            for s in range(4):
+                for h in range(2):
+                    nc.tensor.transpose(
+                        pk[:, h, s, :], k_tile(4 * c + s)[:, P * h : P * h + P], ident_b[:]
+                    )
+
+        def k_out(c):
+            nc.vector.tensor_copy(
+                out=kT[:, :, 512 * c : 512 * c + 512],
+                in_=bank["k", c][:].rearrange("p h s n -> p h (s n)"),
+            )
+
+        def t_transposes(a):
+            pt = psum.tile([P, 2, 4, P], BF16, tag="x", bufs=X_BANKS, name="pt")
+            bank["t", a] = pt
+            for s in range(4):
+                for h in range(2):
+                    nc.tensor.transpose(
+                        pt[:, h, s, :], t_nat[:, 4 * a + s, P * h : P * h + P], ident_b[:]
+                    )
+
+        def t_out(a):
+            nc.vector.tensor_scalar(
+                out=tT[:, :, 512 * a : 512 * a + 512],
+                in0=bank["t", a][:].rearrange("p h s n -> p h (s n)"),
+                scalar1=-2.0,
+                scalar2=None,
+                op0=ALU.mult,
+            )
+
+        zr = {}
+        zm8 = {}
+
+        def scores(x):
+            if x >= BT * NCH:
+                return
+            i, c = x // NCH, x % NCH
+            sp = psum.tile([P, 512], F32, tag="s", bufs=S_BANKS, name="sp")
+            bank["s", x] = sp
+            for s in range(4):
+                m = 4 * c + s
+                nc.tensor.matmul(
+                    sp[:, P * s : P * s + P],
+                    lhsT=kk[:, m : m + 1].to_broadcast([P, P]),
+                    rhs=ident_f[:],
+                    is_transpose=True,
+                    start=(s == 0),
+                    stop=False,
+                )
+            for h in range(2):
+                nc.tensor.matmul(
+                    sp[:],
+                    lhsT=tT[:, h, P * i : P * i + P],
+                    rhs=kT[:, h, 512 * c : 512 * c + 512],
+                    start=False,
+                    stop=(h == 1),
+                )
+
+        def clamp_min(x):
+            i, c = x // NCH, x % NCH
+            if c == 0:
+                zr[i] = work.tile([P, N], F32, tag="zr", bufs=ZR_BUFS, name="zr")
+                zm8[i] = work.tile([P, NCH], F32, tag="zm8", bufs=2, name="zm8")
+            nc.vector.tensor_scalar(
+                out=zr[i][:, 512 * c : 512 * c + 512],
+                in0=bank["s", x][:],
+                scalar1=negtt[:, i : i + 1],
+                scalar2=None,
+                op0=ALU.max,
+                op1=ALU.min,
+                accum_out=zm8[i][:, c : c + 1],
+            )
+
+        def row_min(i):
+            nc.vector.tensor_reduce(out=zmin[:, i : i + 1], in_=zm8[i][:], axis=AX.X, op=ALU.min)
+
+        def root(i):
+            nc.scalar.activation(
+                out=bexp[:, i : i + 1],
+                in_=zmin[:, i : i + 1],
+                func=ACTF.Sqrt,
+                bias=tt256[:, i : i + 1],
+                scale=1.0 / 256.0,
+            )
+            nc.scalar.activation(
+                out=zr[i][:], in_=zr[i][:], func=ACTF.Sqrt, bias=tt[:, i : i + 1], scale=1.0
+            )
+
+        e_sb = {}
+
+        def expo(i):
+            e_sb[i] = work.tile([P, N], BF16, tag="e", bufs=E_BUFS, name="e_sb")
+            nc.scalar.activation(
+                out=e_sb[i][:],
+                in_=zr[i][:],
+                func=ACTF.Exp,
+                bias=bexp[:, i : i + 1],
+                scale=-1.0 / 16.0,
+                accum_out=rsum[:, i : i + 1],
+            )
+
+        egrp = {}
+        ecodes = {}
+        escales = {}
+
+        def e_transposes(j, q):
+            xt = psum.tile([P, 2, 2, P], F32, tag="x", bufs=X_BANKS, name="xt")
+            bank["e", j, q] = xt
+            words = e_sb[j][:].bitcast(F32)
+            for gg in range(2):
+                for u in range(2):
+                    w0 = 256 * (2 * q + gg) + P * u
+                    nc.tensor.transpose(xt[:, gg, u, :], words[:, w0 : w0 + P], ident_f[:])
+
+        def e_out(j, q):
+            if q == 0:
+                egrp[j] = work.tile(
+                    [P, NCH, P, 4], BF16, tag="egrp", bufs=2, name="egrp", align_bytes=64
+                )
+            nc.vector.tensor_copy(
+                out=egrp[j][:].bitcast(F32)[:, 2 * q : 2 * q + 2, :, :],
+                in_=bank["e", j, q][:].rearrange("p g u b -> p g b u"),
+            )
+
+        def e_quantise(j):
+            ecodes[j] = work.tile([P, NCH * P], U32, tag="ecodes", bufs=2, name="ecodes", align_bytes=64)
+            escales[j] = work.tile([P, NCH * P], U8, tag="escales", bufs=2, name="escales", align_bytes=64)
+            nc.vector.quantize_mx(
+                out=ecodes[j][:].bitcast(FP8X4),
+                scales=escales[j][:],
+                in_=egrp[j][:].rearrange("p g b t -> p (g b t)"),
+            )
+
+        def weighted_sum(j):
+            po = psum.tile([P, D], F32, tag="o", bufs=1, name="po")
+            bank["o", j] = po
+            for g in range(NCH):
+                nc.tensor.matmul_mx(
+                    out=po[:],
+                    lhsT=ecodes[j][:, P * g : P * g + P].bitcast(FP8X4),
+                    lhsT_scale=escales[j][:, P * g : P * g + P],
+                    rhs=fcodes[:, g, :].bitcast(FP8X4),
+                    rhs_scale=fscales[:, g, :],
+                    start=(g == 0),
+                    stop=(g == NCH - 1),
+                )
+
+        def finish(j):
+            nc.vector.reciprocal(rinv[:, j : j + 1], rsum[:, j : j + 1])
+            o_sb = work.tile([P, D], F32, tag="o_sb", bufs=2, name="o_sb")
+            nc.vector.tensor_scalar(
+                out=o_sb[:], in0=bank["o", j][:], scalar1=rinv[:, j : j + 1], scalar2=None, op0=ALU.mult
+            )
+            nc.sync.dma_start(out=out[P * j : P * j + P, :], in_=o_sb[:])
+
+        sgrp = {}
+        scodes = {}
+        sscales = {}
+        fgrp = {}
+
+        def w_transposes():
+            xw = psum.tile([P, 2, 2, P], F32, tag="x", bufs=X_BANKS, name="xw")
+            bank["w"] = xw
+            words = wf_nat[:].bitcast(F32)
+            for h in range(2):
+                for u in range(2):
+                    nc.tensor.transpose(xw[:, h, u, :], words[:, h, P * u : P * u + P], ident_f[:])
+
+        def w_out():
+            nc.vector.tensor_copy(
+                out=wgrp[:].bitcast(F32).rearrange("p (h d) u -> p h d u", h=2),
+                in_=bank["w"][:].rearrange("p h u d -> p h d u"),
+            )
+
+        def w_quantise():
+            nc.vector.quantize_mx(
+                out=wcodes[:].bitcast(FP8X4),
+                scales=wscales[:],
+                in_=wgrp[:].rearrange("p d t -> p (d t)"),
+            )
+
+        def s_transposes(g, half):
+            xs = psum.tile([P, 2, 2, P], F32, tag="x", bufs=X_BANKS, name="xs")
+            bank["src", g, half] = xs
+            words = src[g][:].bitcast(F32)
+            for tl in range(2):
+                for u in range(2):
+                    nc.tensor.transpose(
+                        xs[:, tl, u, :], words[:, 2 * half + tl, P * u : P * u + P], ident_f[:]
+                    )
+
+        def s_out(g, half):
+            if half == 0:
+                sgrp[g] = work.tile([P, 4, P, 4], BF16, tag="sgrp", bufs=2, name="sgrp", align_bytes=64)
+            nc.vector.tensor_copy(
+                out=sgrp[g][:].bitcast(F32)[:, 2 * half : 2 * half + 2, :, :],
+                in_=bank["src", g, half][:].rearrange("p t u n -> p t n u"),
+            )
+            if half == 1 and g + 2 < NCH:
+                load_src(g + 2)
+
+        def s_quantise(g):
+            scodes[g] = work.tile([P, 4 * P], U32, tag="scodes", bufs=2, name="scodes", align_bytes=64)
+            sscales[g] = work.tile([P, 4 * P], U8, tag="sscales", bufs=2, name="sscales", align_bytes=64)
+            nc.vector.quantize_mx(
+                out=scodes[g][:].bitcast(FP8X4),
+                scales=sscales[g][:],
+                in_=sgrp[g][:].rearrange("p t n k -> p (t n k)"),
+            )
+
+        def f_matmuls(g, dh):
+            fb = psum.tile([P, 4, P], F32, tag="x", bufs=X_BANKS, name="fb")
+            bank["f", g, dh] = fb
+            for t in range(4):
+                nc.tensor.matmul_mx(
+                    out=fb[:, t, :],
+                    lhsT=scodes[g][:, P * t : P * t + P].bitcast(FP8X4),
+                    lhsT_scale=sscales[g][:, P * t : P * t + P],
+                    rhs=wcodes[:, P * dh : P * dh + P].bitcast(FP8X4),
+                    rhs_scale=wscales[:, P * dh : P * dh + P],
+                    start=True,
+                    stop=True,
+                )
+
+        def f_out(g, dh):
+            if dh == 0:
+                fgrp[g] = work.tile([P, D, 4], BF16, tag="fgrp", bufs=2, name="fgrp", align_bytes=64)
+            nc.vector.tensor_copy(
+                out=fgrp[g][:, P * dh : P * dh + P, :],
+                in_=bank["f", g, dh][:].rearrange("p t d -> p d t"),
+            )
+
+        def f_quantise(g):
+            nc.vector.quantize_mx(
+                out=fcodes[:, g, :].bitcast(FP8X4),
+                scales=fscales[:, g, :],
+                in_=fgrp[g][:].rearrange("p d t -> p (d t)"),
+            )
+
+        steps = []
+
+        def step(body, ahead=None):
+            steps.append((ahead, body))
+
+        def distances(i, extra=None):
+            for c in range(NCH):
+                x = NCH * i + c
+                step(lambda x=x: (clamp_min(x), scores(x + S_BANKS)))
+                if extra is not None and c in extra:
+                    for s in extra[c]:
+                        steps.append(s)
+            step(lambda i=i: row_min(i))
+
+        def posts(j0, exps):
+            for r in range(5):
+                j = j0 + r
+                if r < 4:
+                    for q in range(4):
+                        step(lambda j=j, q=q: e_out(j, q), lambda j=j, q=q: e_transposes(j, q))
+                    if exps:
+                        step(lambda j=j: expo(j + 4))
+                if r >= 1:
+                    step(lambda j=j: e_quantise(j - 1))
+                if r >= 2:
+                    step(lambda j=j: finish(j - 2))
+                if r >= 1:
+                    step(lambda j=j: weighted_sum(j - 1))
+
+        def prepare_f():
+            def a_steps(g):
+                for half in range(2):
+                    step(lambda g=g, half=half: s_out(g, half), lambda g=g, half=half: s_transposes(g, half))
+
+            step(w_out, w_transposes)
+            a_steps(0)
+            step(w_quantise)
+            step(lambda: s_quantise(0))
+            for g in range(NCH):
+                if g + 1 < NCH:
+                    a_steps(g + 1)
+                if g >= 1:
+                    step(lambda g=g: f_quantise(g - 1))
+                if g + 1 < NCH:
+                    step(lambda g=g: s_quantise(g + 1))
+                for dh in range(2):
+                    step(lambda g=g, dh=dh: f_out(g, dh), lambda g=g, dh=dh: f_matmuls(g, dh))
+            step(lambda: f_quantise(NCH - 1))
+
+        for i in range(4):
+            square_t(i)
+        norms_t(0, 4)
+        for c in range(NCH):
+            step(
+                lambda c=c: (k_out(c), [square_k(4 * c + s) for s in range(4)]),
+                lambda c=c: k_transposes(c),
+            )
+            if c == 0:
+                step(lambda: t_out(0), lambda: t_transposes(0))
+            step(lambda c=c: scores(c))
+            if c >= 1:
+                step(lambda c=c: clamp_min(c - 1))
+        step(lambda: (scores(8), scores(9), scores(10), clamp_min(7), scores(11), row_min(0)))
+
+        for i in range(1, 4):
+            step(lambda i=i: (root(i - 1), [square_t(4 * i + s) for s in range(4)]))
+            distances(i, {3: [(lambda i=i: t_transposes(i), lambda i=i: t_out(i))]})
+        step(lambda: (root(3), norms_t(4, BT)))
+        distances(4)
+        distances(5)
+        step(lambda: expo(0))
+        distances(6)
+        step(lambda: expo(1))
+        distances(7)
+        step(lambda: (expo(2), expo(3), root(4), root(5), root(6), root(7)))
+        prepare_f()
+        for j0 in (0, 4):
+            posts(j0, True)
+            for i in range(j0 + 8, j0 + 12):
+                distances(i, {1: [(None, lambda j0=j0: finish(j0 + 3))]} if i == j0 + 8 else None)
+                step(lambda i=i: root(i))
+        posts(8, True)
+        step(lambda: finish(11))
+        posts(12, False)
+        step(lambda: finish(15))
+
+        for idx in range(-AHEAD, len(steps)):
+            if idx >= 0:
+                steps[idx][1]()
+            if idx + AHEAD < len(steps) and steps[idx + AHEAD][0] is not None:
+                steps[idx + AHEAD][0]()

@@ -23,7 +23,6 @@ ZR_BUFS = 6
 E_BUFS = 4
 S_BANKS = 4
 X_BANKS = 3
-AHEAD = 2
 PHASE = 4
 
 
@@ -156,30 +155,43 @@ def tile_kanadjunction_pa_kernel(tc, source, target, k_right, WF_right, out):
         zr = {}
         zm8 = {}
 
-        def scores(x):
-            if x >= BT * NCH:
-                return
+        def fold(x, s):
+            c = x % NCH
+            if s == 0:
+                bank["s", x] = psum.tile([P, 512], F32, tag="s", bufs=S_BANKS, name="sp")
+            m = 4 * c + s
+            nc.tensor.matmul(
+                bank["s", x][:, P * s : P * s + P],
+                lhsT=kk[:, m : m + 1].to_broadcast([P, P]),
+                rhs=ident_f[:],
+                is_transpose=True,
+                start=(s == 0),
+                stop=False,
+            )
+
+        def product(x, h):
             i, c = x // NCH, x % NCH
-            sp = psum.tile([P, 512], F32, tag="s", bufs=S_BANKS, name="sp")
-            bank["s", x] = sp
+            nc.tensor.matmul(
+                bank["s", x][:],
+                lhsT=tT[:, h, P * i : P * i + P],
+                rhs=kT[:, h, 512 * c : 512 * c + 512],
+                start=False,
+                stop=(h == 1),
+            )
+
+        def whole_bank(x):
             for s in range(4):
-                m = 4 * c + s
-                nc.tensor.matmul(
-                    sp[:, P * s : P * s + P],
-                    lhsT=kk[:, m : m + 1].to_broadcast([P, P]),
-                    rhs=ident_f[:],
-                    is_transpose=True,
-                    start=(s == 0),
-                    stop=False,
-                )
+                fold(x, s)
             for h in range(2):
-                nc.tensor.matmul(
-                    sp[:],
-                    lhsT=tT[:, h, P * i : P * i + P],
-                    rhs=kT[:, h, 512 * c : 512 * c + 512],
-                    start=False,
-                    stop=(h == 1),
-                )
+                product(x, h)
+
+        def scores(x):
+            for h in range(2):
+                if x + 1 < BT * NCH:
+                    fold(x + 1, 2 * h)
+                    fold(x + 1, 2 * h + 1)
+                if x < BT * NCH:
+                    product(x, h)
 
         def clamp_min(x):
             i, c = x // NCH, x % NCH
@@ -272,7 +284,7 @@ def tile_kanadjunction_pa_kernel(tc, source, target, k_right, WF_right, out):
 
         def finish(j):
             nc.vector.reciprocal(rinv[:, j : j + 1], rsum[:, j : j + 1])
-            o_sb = work.tile([P, D], F32, tag="o_sb", bufs=2, name="o_sb")
+            o_sb = work.tile([P, D], F32, tag="o_sb", bufs=4, name="o_sb")
             nc.vector.tensor_scalar(
                 out=o_sb[:], in0=bank["o", j][:], scalar1=rinv[:, j : j + 1], scalar2=None, op0=ALU.mult
             )
@@ -364,13 +376,13 @@ def tile_kanadjunction_pa_kernel(tc, source, target, k_right, WF_right, out):
 
         steps = []
 
-        def step(body, ahead=None):
-            steps.append((ahead, body))
+        def step(body, ahead=None, ready=None):
+            steps.append((ahead, body, ready))
 
         def distances(i, extra=None):
             for c in range(NCH):
                 x = NCH * i + c
-                step(lambda x=x: (clamp_min(x), scores(x + S_BANKS)))
+                step(lambda x=x: (clamp_min(x), scores(x + S_BANKS - 1)))
                 if extra is not None and c in extra:
                     for s in extra[c]:
                         steps.append(s)
@@ -381,7 +393,7 @@ def tile_kanadjunction_pa_kernel(tc, source, target, k_right, WF_right, out):
                 j = j0 + r
                 if r < 4:
                     for q in range(4):
-                        step(lambda j=j, q=q: e_out(j, q), lambda j=j, q=q: e_transposes(j, q))
+                        step(lambda j=j, q=q: e_out(j, q), lambda j=j, q=q: e_transposes(j, q), lambda j=j: j in e_sb)
                     if exps:
                         step(lambda j=j: expo(j + 4))
                 if r >= 1:
@@ -394,7 +406,7 @@ def tile_kanadjunction_pa_kernel(tc, source, target, k_right, WF_right, out):
         def prepare_f():
             def a_steps(g):
                 for half in range(2):
-                    step(lambda g=g, half=half: s_out(g, half), lambda g=g, half=half: s_transposes(g, half))
+                    step(lambda g=g, half=half: s_out(g, half), lambda g=g, half=half: s_transposes(g, half), lambda g=g: g in src)
 
             step(w_out, w_transposes)
             a_steps(0)
@@ -408,7 +420,7 @@ def tile_kanadjunction_pa_kernel(tc, source, target, k_right, WF_right, out):
                 if g + 1 < NCH:
                     step(lambda g=g: s_quantise(g + 1))
                 for dh in range(2):
-                    step(lambda g=g, dh=dh: f_out(g, dh), lambda g=g, dh=dh: f_matmuls(g, dh))
+                    step(lambda g=g, dh=dh: f_out(g, dh), lambda g=g, dh=dh: f_matmuls(g, dh), lambda g=g: g in scodes)
             step(lambda: f_quantise(NCH - 1))
 
         for i in range(4):
@@ -421,14 +433,14 @@ def tile_kanadjunction_pa_kernel(tc, source, target, k_right, WF_right, out):
             )
             if c == 0:
                 step(lambda: t_out(0), lambda: t_transposes(0))
-            step(lambda c=c: scores(c))
+            step(lambda c=c: whole_bank(c))
             if c >= 1:
                 step(lambda c=c: clamp_min(c - 1))
-        step(lambda: (scores(8), scores(9), scores(10), clamp_min(7), scores(11), row_min(0)))
+        step(lambda: ([fold(8, s) for s in range(4)], scores(8), scores(9), clamp_min(7), scores(10), row_min(0)))
 
         for i in range(1, 4):
             step(lambda i=i: (root(i - 1), [square_t(4 * i + s) for s in range(4)]))
-            distances(i, {3: [(lambda i=i: t_transposes(i), lambda i=i: t_out(i))]})
+            distances(i, {3: [(lambda i=i: t_transposes(i), lambda i=i: t_out(i), None)]})
         step(lambda: (root(3), norms_t(4, BT)))
         distances(4)
         distances(5)
@@ -441,15 +453,28 @@ def tile_kanadjunction_pa_kernel(tc, source, target, k_right, WF_right, out):
         for j0 in (0, 4):
             posts(j0, True)
             for i in range(j0 + 8, j0 + 12):
-                distances(i, {1: [(None, lambda j0=j0: finish(j0 + 3))]} if i == j0 + 8 else None)
+                distances(i, {1: [(None, lambda j0=j0: finish(j0 + 3), None)]} if i == j0 + 8 else None)
                 step(lambda i=i: root(i))
         posts(8, True)
         step(lambda: finish(11))
         posts(12, False)
         step(lambda: finish(15))
 
-        for idx in range(-AHEAD, len(steps)):
-            if idx >= 0:
-                steps[idx][1]()
-            if idx + AHEAD < len(steps) and steps[idx + AHEAD][0] is not None:
-                steps[idx + AHEAD][0]()
+        fed = [idx for idx in range(len(steps)) if steps[idx][0] is not None]
+        state = {"next": 0, "open": 0}
+
+        def feed():
+            while state["next"] < len(fed) and state["open"] < X_BANKS:
+                ahead, body, ready = steps[fed[state["next"]]]
+                if ready is not None and not ready():
+                    break
+                ahead()
+                state["next"] += 1
+                state["open"] += 1
+
+        feed()
+        for ahead, body, ready in steps:
+            body()
+            if ahead is not None:
+                state["open"] -= 1
+            feed()

@@ -23,7 +23,11 @@ ZR_BUFS = 6
 E_BUFS = 4
 S_BANKS = 4
 X_BANKS = 3
-PHASE = 4
+PHASES = (4, 4, 3, 3, 2)
+LEAD = 6
+PREP_PER_TILE = (0, 13, 13, 13, 13, 4)
+POST_START = 44
+POST_NUM, POST_DEN = 3, 4
 
 
 def tile_kanadjunction_pa_kernel(tc, source, target, k_right, WF_right, out):
@@ -375,96 +379,147 @@ def tile_kanadjunction_pa_kernel(tc, source, target, k_right, WF_right, out):
             )
 
         steps = []
+        seen = set()
+
+        act_queue = []
+        first = 0
+        for size in PHASES:
+            act_queue.extend([("root", t) for t in range(first, first + size)])
+            act_queue.extend([("exp", t) for t in range(first, first + size)])
+            first += size
+        act_state = {"next": 0}
+
+        def pump_act():
+            while act_state["next"] < len(act_queue):
+                kind, t = act_queue[act_state["next"]]
+                if kind == "root":
+                    if ("min", t) not in seen:
+                        break
+                    root(t)
+                    if t < 3:
+                        for s in range(4):
+                            square_t(4 * t + 4 + s)
+                else:
+                    if t >= E_BUFS and ("turned", t - E_BUFS) not in seen:
+                        break
+                    expo(t)
+                act_state["next"] += 1
 
         def step(body, ahead=None, ready=None):
             steps.append((ahead, body, ready))
 
-        def distances(i, extra=None):
-            for c in range(NCH):
-                x = NCH * i + c
-                step(lambda x=x: (clamp_min(x), scores(x + S_BANKS - 1)))
-                if extra is not None and c in extra:
-                    for s in extra[c]:
-                        steps.append(s)
-            step(lambda i=i: row_min(i))
+        def mark(key):
+            seen.add(key)
 
-        def posts(j0, exps):
-            for r in range(5):
-                j = j0 + r
-                if r < 4:
-                    for q in range(4):
-                        step(lambda j=j, q=q: e_out(j, q), lambda j=j, q=q: e_transposes(j, q), lambda j=j: j in e_sb)
-                    if exps:
-                        step(lambda j=j: expo(j + 4))
-                if r >= 1:
-                    step(lambda j=j: e_quantise(j - 1))
-                if r >= 2:
-                    step(lambda j=j: finish(j - 2))
-                if r >= 1:
-                    step(lambda j=j: weighted_sum(j - 1))
+        prep = []
 
-        def prepare_f():
-            def a_steps(g):
-                for half in range(2):
-                    step(lambda g=g, half=half: s_out(g, half), lambda g=g, half=half: s_transposes(g, half), lambda g=g: g in src)
+        def prep_item(body, ahead=None, ready=None):
+            prep.append((ahead, body, ready))
 
-            step(w_out, w_transposes)
-            a_steps(0)
-            step(w_quantise)
-            step(lambda: s_quantise(0))
-            for g in range(NCH):
-                if g + 1 < NCH:
-                    a_steps(g + 1)
-                if g >= 1:
-                    step(lambda g=g: f_quantise(g - 1))
-                if g + 1 < NCH:
-                    step(lambda g=g: s_quantise(g + 1))
-                for dh in range(2):
-                    step(lambda g=g, dh=dh: f_out(g, dh), lambda g=g, dh=dh: f_matmuls(g, dh), lambda g=g: g in scodes)
-            step(lambda: f_quantise(NCH - 1))
+        def source_items(g):
+            for half in range(2):
+                prep_item(
+                    lambda g=g, half=half: s_out(g, half),
+                    lambda g=g, half=half: s_transposes(g, half),
+                    lambda g=g: g in src,
+                )
+
+        prep_item(lambda: t_out(1), lambda: t_transposes(1))
+        prep_item(w_out, w_transposes)
+        source_items(0)
+        prep_item(w_quantise)
+        prep_item(lambda: s_quantise(0))
+        for g in range(NCH):
+            if g + 1 < NCH:
+                source_items(g + 1)
+            if g >= 1:
+                prep_item(lambda g=g: f_quantise(g - 1))
+            if g + 1 < NCH:
+                prep_item(lambda g=g: s_quantise(g + 1))
+            for dh in range(2):
+                prep_item(
+                    lambda g=g, dh=dh: f_out(g, dh),
+                    lambda g=g, dh=dh: f_matmuls(g, dh),
+                    lambda g=g: g in scodes,
+                )
+            if g in (1, 3):
+                a = (g + 3) // 2
+                prep_item(lambda a=a: t_out(a), lambda a=a: t_transposes(a))
+        prep_item(lambda: f_quantise(NCH - 1))
+
+        post = []
+        for j in range(BT):
+            for q in range(4):
+                post.append(
+                    (
+                        lambda j=j, q=q: e_transposes(j, q),
+                        lambda j=j, q=q: (e_out(j, q), mark(("turned", j)) if q == 3 else None),
+                        lambda j=j: j in e_sb,
+                    )
+                )
+                if q == 1 and j >= 1:
+                    post.append((None, lambda j=j: finish(j - 1), None))
+            post.append((None, lambda j=j: (e_quantise(j), weighted_sum(j)), None))
+        post.append((None, lambda: finish(BT - 1), None))
 
         for i in range(4):
             square_t(i)
         norms_t(0, 4)
-        for c in range(NCH):
+
+        def key_step(c):
             step(
                 lambda c=c: (k_out(c), [square_k(4 * c + s) for s in range(4)]),
                 lambda c=c: k_transposes(c),
             )
             if c == 0:
                 step(lambda: t_out(0), lambda: t_transposes(0))
+
+        for c in range(3):
+            key_step(c)
+        for c in range(NCH):
             step(lambda c=c: whole_bank(c))
+            if c + 3 < NCH:
+                key_step(c + 3)
             if c >= 1:
                 step(lambda c=c: clamp_min(c - 1))
-        step(lambda: ([fold(8, s) for s in range(4)], scores(8), scores(9), clamp_min(7), scores(10), row_min(0)))
+        step(
+            lambda: (
+                [fold(8, s) for s in range(4)],
+                scores(8),
+                scores(9),
+                clamp_min(7),
+                scores(10),
+                row_min(0),
+                mark(("min", 0)),
+            )
+        )
 
-        for i in range(1, 4):
-            step(lambda i=i: (root(i - 1), [square_t(4 * i + s) for s in range(4)]))
-            distances(i, {3: [(lambda i=i: t_transposes(i), lambda i=i: t_out(i), None)]})
-        step(lambda: (root(3), norms_t(4, BT)))
-        distances(4)
-        distances(5)
-        step(lambda: expo(0))
-        distances(6)
-        step(lambda: expo(1))
-        distances(7)
-        step(lambda: (expo(2), expo(3), root(4), root(5), root(6), root(7)))
-        prepare_f()
-        for j0 in (0, 4):
-            posts(j0, True)
-            for i in range(j0 + 8, j0 + 12):
-                distances(i, {1: [(None, lambda j0=j0: finish(j0 + 3), None)]} if i == j0 + 8 else None)
-                step(lambda i=i: root(i))
-        posts(8, True)
-        step(lambda: finish(11))
-        posts(12, False)
-        step(lambda: finish(15))
+        taken = {"prep": 0, "post": 0}
+        for x in range(NCH, BT * NCH):
+            i, c = x // NCH, x % NCH
+            if x == 30:
+                step(lambda: norms_t(4, BT))
+            step(lambda x=x: (clamp_min(x), scores(x + S_BANKS - 1)))
+            if c == NCH - 1:
+                step(lambda i=i: (row_min(i), mark(("min", i))))
+            share = PREP_PER_TILE[i] if i < len(PREP_PER_TILE) else 0
+            for r in range(share * (c + 1) // NCH - share * c // NCH):
+                if taken["prep"] < len(prep):
+                    steps.append(prep[taken["prep"]])
+                    taken["prep"] += 1
+            if x >= POST_START:
+                due = (x - POST_START + 1) * POST_NUM // POST_DEN
+                while taken["post"] < min(due, len(post)):
+                    steps.append(post[taken["post"]])
+                    taken["post"] += 1
+        steps.extend(prep[taken["prep"] :])
+        steps.extend(post[taken["post"] :])
 
         fed = [idx for idx in range(len(steps)) if steps[idx][0] is not None]
         state = {"next": 0, "open": 0}
 
-        def feed():
-            while state["next"] < len(fed) and state["open"] < X_BANKS:
+        def feed(now):
+            while state["next"] < len(fed) and state["open"] < X_BANKS and fed[state["next"]] - now <= LEAD:
                 ahead, body, ready = steps[fed[state["next"]]]
                 if ready is not None and not ready():
                     break
@@ -472,9 +527,11 @@ def tile_kanadjunction_pa_kernel(tc, source, target, k_right, WF_right, out):
                 state["next"] += 1
                 state["open"] += 1
 
-        feed()
-        for ahead, body, ready in steps:
+        feed(-1)
+        for now in range(len(steps)):
+            ahead, body, ready = steps[now]
             body()
+            pump_act()
             if ahead is not None:
                 state["open"] -= 1
-            feed()
+            feed(now)

@@ -19,7 +19,7 @@ BT = B // P
 NCH = N // 512
 FLOPS = 2 * (N * C * D + 2 * B * N * E)
 
-ZR_BUFS = 6
+ZR_BUFS = 5
 E_BUFS = 4
 S_BANKS = 4
 X_BANKS = 3
@@ -50,6 +50,7 @@ def tile_kanadjunction_pa_kernel(tc, source, target, k_right, WF_right, out):
         kT = keep.tile([P, 2, N], BF16, name="kT")
         tT = keep.tile([P, 2, B], BF16, name="tT")
         kk = keep.tile([P, NT], F32, name="kk")
+        kk_wide = keep.tile([P, NT, P], F32, name="kk_wide")
         tt = keep.tile([P, BT], F32, name="tt")
         negtt = keep.tile([P, BT], F32, name="negtt")
         tt256 = keep.tile([P, BT], F32, name="tt256")
@@ -113,6 +114,12 @@ def tile_kanadjunction_pa_kernel(tc, source, target, k_right, WF_right, out):
                 out=junk[:], in_=k_tile(m), func=ACTF.Square, accum_out=kk[:, m : m + 1]
             )
 
+        def widen_k(c):
+            nc.vector.tensor_copy(
+                out=kk_wide[:, 4 * c : 4 * c + 4, :],
+                in_=kk[:, 4 * c : 4 * c + 4].unsqueeze(2).to_broadcast([P, 4, P]),
+            )
+
         def norms_t(a, b):
             nc.vector.tensor_scalar(
                 out=negtt[:, a:b], in0=tt[:, a:b], scalar1=-1.0, scalar2=None, op0=ALU.mult
@@ -166,7 +173,7 @@ def tile_kanadjunction_pa_kernel(tc, source, target, k_right, WF_right, out):
             m = 4 * c + s
             nc.tensor.matmul(
                 bank["s", x][:, P * s : P * s + P],
-                lhsT=kk[:, m : m + 1].to_broadcast([P, P]),
+                lhsT=kk_wide[:, m, :],
                 rhs=ident_f[:],
                 is_transpose=True,
                 start=(s == 0),
@@ -477,7 +484,7 @@ def tile_kanadjunction_pa_kernel(tc, source, target, k_right, WF_right, out):
         for c in range(3):
             key_step(c)
         for c in range(NCH):
-            step(lambda c=c: whole_bank(c))
+            step(lambda c=c: (widen_k(c), whole_bank(c)))
             if c + 3 < NCH:
                 key_step(c + 3)
             if c >= 1:

@@ -19,11 +19,11 @@ BT = B // P
 NCH = N // 512
 FLOPS = 2 * (N * C * D + 2 * B * N * E)
 
-ZR_BUFS = 5
+ZR_BUFS = 6
 E_BUFS = 4
 S_BANKS = 4
 X_BANKS = 3
-PHASES = (4, 4, 3, 3, 2)
+PHASES = (1, 2, 3, 3, 3, 4)
 LEAD = 6
 PREP_PER_TILE = (0, 13, 13, 13, 13, 4)
 POST_START = 44
@@ -50,7 +50,6 @@ def tile_kanadjunction_pa_kernel(tc, source, target, k_right, WF_right, out):
         kT = keep.tile([P, 2, N], BF16, name="kT")
         tT = keep.tile([P, 2, B], BF16, name="tT")
         kk = keep.tile([P, NT], F32, name="kk")
-        kk_wide = keep.tile([P, NT, P], F32, name="kk_wide")
         tt = keep.tile([P, BT], F32, name="tt")
         negtt = keep.tile([P, BT], F32, name="negtt")
         tt256 = keep.tile([P, BT], F32, name="tt256")
@@ -114,12 +113,6 @@ def tile_kanadjunction_pa_kernel(tc, source, target, k_right, WF_right, out):
                 out=junk[:], in_=k_tile(m), func=ACTF.Square, accum_out=kk[:, m : m + 1]
             )
 
-        def widen_k(c):
-            nc.vector.tensor_copy(
-                out=kk_wide[:, 4 * c : 4 * c + 4, :],
-                in_=kk[:, 4 * c : 4 * c + 4].unsqueeze(2).to_broadcast([P, 4, P]),
-            )
-
         def norms_t(a, b):
             nc.vector.tensor_scalar(
                 out=negtt[:, a:b], in0=tt[:, a:b], scalar1=-1.0, scalar2=None, op0=ALU.mult
@@ -173,7 +166,7 @@ def tile_kanadjunction_pa_kernel(tc, source, target, k_right, WF_right, out):
             m = 4 * c + s
             nc.tensor.matmul(
                 bank["s", x][:, P * s : P * s + P],
-                lhsT=kk_wide[:, m, :],
+                lhsT=kk[:, m : m + 1].to_broadcast([P, P]),
                 rhs=ident_f[:],
                 is_transpose=True,
                 start=(s == 0),
@@ -484,7 +477,7 @@ def tile_kanadjunction_pa_kernel(tc, source, target, k_right, WF_right, out):
         for c in range(3):
             key_step(c)
         for c in range(NCH):
-            step(lambda c=c: (widen_k(c), whole_bank(c)))
+            step(lambda c=c: whole_bank(c))
             if c + 3 < NCH:
                 key_step(c + 3)
             if c >= 1:

@@ -25,6 +25,7 @@ S_BANKS = 4
 X_BANKS = 3
 PHASES = (1, 2, 3, 3, 3, 4)
 LEAD = 6
+SPLIT_ROOTS = 3
 PREP_PER_TILE = (0, 13, 13, 13, 13, 4)
 POST_START = 44
 POST_NUM, POST_DEN = 3, 4
@@ -49,15 +50,20 @@ def tile_kanadjunction_pa_kernel(tc, source, target, k_right, WF_right, out):
 
         kT = keep.tile([P, 2, N], BF16, name="kT")
         tT = keep.tile([P, 2, B], BF16, name="tT")
-        kk = keep.tile([P, NT], F32, name="kk")
+        kk_s = keep.tile([P, NT], F32, name="kk_s")
+        kk_v = keep.tile([P, NT], F32, name="kk_v")
         tt = keep.tile([P, BT], F32, name="tt")
         negtt = keep.tile([P, BT], F32, name="negtt")
         tt256 = keep.tile([P, BT], F32, name="tt256")
         zmin = keep.tile([P, BT], F32, name="zmin")
+        barg = keep.tile([P, BT], F32, name="barg")
         bexp = keep.tile([P, BT], F32, name="bexp")
+        rsum_last = keep.tile([P, 2], F32, name="rsum_last")
+        rsum_both = keep.tile([P, 1], F32, name="rsum_both")
         rsum = keep.tile([P, BT], F32, name="rsum")
         rinv = keep.tile([P, BT], F32, name="rinv")
         junk = keep.tile([P, E], BF16, name="junk")
+        junk_v = keep.tile([P, E], F32, name="junk_v")
         fcodes = keep.tile([P, NCH, D], U32, name="fcodes", align_bytes=64)
         fscales = keep.tile([P, NCH, D], U8, name="fscales", align_bytes=64)
         wcodes = keep.tile([P, D], U32, name="wcodes", align_bytes=64)
@@ -103,15 +109,22 @@ def tile_kanadjunction_pa_kernel(tc, source, target, k_right, WF_right, out):
         def k_tile(m):
             return k_nat[m // 16][:, m % 16, :]
 
-        def square_t(i):
-            nc.scalar.activation(
-                out=junk[:], in_=t_nat[:, i, :], func=ACTF.Square, accum_out=tt[:, i : i + 1]
+        def vector_norm(rows, total):
+            nc.vector.scalar_tensor_tensor(
+                out=junk_v[:], in0=rows, scalar=1.0, in1=rows, op0=ALU.mult, op1=ALU.mult, accum_out=total
             )
 
+        def square_t(i):
+            vector_norm(t_nat[:, i, :], tt[:, i : i + 1])
+
+        def kk_column(m):
+            return (kk_v if m % 4 == 3 else kk_s)[:, m : m + 1]
+
         def square_k(m):
-            nc.scalar.activation(
-                out=junk[:], in_=k_tile(m), func=ACTF.Square, accum_out=kk[:, m : m + 1]
-            )
+            if m % 4 == 3:
+                vector_norm(k_tile(m), kk_column(m))
+            else:
+                nc.scalar.activation(out=junk[:], in_=k_tile(m), func=ACTF.Square, accum_out=kk_column(m))
 
         def norms_t(a, b):
             nc.vector.tensor_scalar(
@@ -166,7 +179,7 @@ def tile_kanadjunction_pa_kernel(tc, source, target, k_right, WF_right, out):
             m = 4 * c + s
             nc.tensor.matmul(
                 bank["s", x][:, P * s : P * s + P],
-                lhsT=kk[:, m : m + 1].to_broadcast([P, P]),
+                lhsT=kk_column(m).to_broadcast([P, P]),
                 rhs=ident_f[:],
                 is_transpose=True,
                 start=(s == 0),
@@ -215,30 +228,39 @@ def tile_kanadjunction_pa_kernel(tc, source, target, k_right, WF_right, out):
         def row_min(i):
             nc.vector.tensor_reduce(out=zmin[:, i : i + 1], in_=zm8[i][:], axis=AX.X, op=ALU.min)
 
-        def root(i):
+        def root(i, lo, hi):
             nc.scalar.activation(
-                out=bexp[:, i : i + 1],
-                in_=zmin[:, i : i + 1],
-                func=ACTF.Sqrt,
-                bias=tt256[:, i : i + 1],
-                scale=1.0 / 256.0,
+                out=zr[i][:, lo:hi], in_=zr[i][:, lo:hi], func=ACTF.Sqrt, bias=tt[:, i : i + 1], scale=1.0
             )
-            nc.scalar.activation(
-                out=zr[i][:], in_=zr[i][:], func=ACTF.Sqrt, bias=tt[:, i : i + 1], scale=1.0
+
+        def shifts(a, b):
+            nc.vector.scalar_tensor_tensor(
+                out=barg[:, a:b],
+                in0=zmin[:, a:b],
+                scalar=1.0 / 256.0,
+                in1=tt256[:, a:b],
+                op0=ALU.mult,
+                op1=ALU.add,
             )
+            nc.scalar.activation(out=bexp[:, a:b], in_=barg[:, a:b], func=ACTF.Sqrt)
 
         e_sb = {}
 
         def expo(i):
             e_sb[i] = work.tile([P, N], BF16, tag="e", bufs=E_BUFS, name="e_sb")
-            nc.scalar.activation(
-                out=e_sb[i][:],
-                in_=zr[i][:],
-                func=ACTF.Exp,
-                bias=bexp[:, i : i + 1],
-                scale=-1.0 / 16.0,
-                accum_out=rsum[:, i : i + 1],
-            )
+            if i < BT - 1:
+                pieces = [(0, N, rsum[:, i : i + 1])]
+            else:
+                pieces = [(0, N // 2, rsum_last[:, 0:1]), (N // 2, N, rsum_last[:, 1:2])]
+            for lo, hi, total in pieces:
+                nc.scalar.activation(
+                    out=e_sb[i][:, lo:hi],
+                    in_=zr[i][:, lo:hi],
+                    func=ACTF.Exp,
+                    bias=bexp[:, i : i + 1],
+                    scale=-1.0 / 16.0,
+                    accum_out=total,
+                )
 
         egrp = {}
         ecodes = {}
@@ -263,19 +285,21 @@ def tile_kanadjunction_pa_kernel(tc, source, target, k_right, WF_right, out):
                 in_=bank["e", j, q][:].rearrange("p g u b -> p g b u"),
             )
 
-        def e_quantise(j):
-            ecodes[j] = work.tile([P, NCH * P], U32, tag="ecodes", bufs=2, name="ecodes", align_bytes=64)
-            escales[j] = work.tile([P, NCH * P], U8, tag="escales", bufs=2, name="escales", align_bytes=64)
+        def e_quantise(j, g0, g1):
+            if g0 == 0:
+                ecodes[j] = work.tile([P, NCH * P], U32, tag="ecodes", bufs=2, name="ecodes", align_bytes=64)
+                escales[j] = work.tile([P, NCH * P], U8, tag="escales", bufs=2, name="escales", align_bytes=64)
             nc.vector.quantize_mx(
-                out=ecodes[j][:].bitcast(FP8X4),
-                scales=escales[j][:],
-                in_=egrp[j][:].rearrange("p g b t -> p (g b t)"),
+                out=ecodes[j][:, P * g0 : P * g1].bitcast(FP8X4),
+                scales=escales[j][:, P * g0 : P * g1],
+                in_=egrp[j][:, g0:g1, :, :].rearrange("p g b t -> p (g b t)"),
             )
 
-        def weighted_sum(j):
-            po = psum.tile([P, D], F32, tag="o", bufs=1, name="po")
-            bank["o", j] = po
-            for g in range(NCH):
+        def weighted_sum(j, g0, g1):
+            if g0 == 0:
+                bank["o", j] = psum.tile([P, D], F32, tag="o", bufs=1, name="po")
+            po = bank["o", j]
+            for g in range(g0, g1):
                 nc.tensor.matmul_mx(
                     out=po[:],
                     lhsT=ecodes[j][:, P * g : P * g + P].bitcast(FP8X4),
@@ -287,7 +311,11 @@ def tile_kanadjunction_pa_kernel(tc, source, target, k_right, WF_right, out):
                 )
 
         def finish(j):
-            nc.vector.reciprocal(rinv[:, j : j + 1], rsum[:, j : j + 1])
+            if j < BT - 1:
+                nc.vector.reciprocal(rinv[:, j : j + 1], rsum[:, j : j + 1])
+            else:
+                nc.vector.tensor_reduce(out=rsum_both[:], in_=rsum_last[:], axis=AX.X, op=ALU.add)
+                nc.vector.reciprocal(rinv[:, j : j + 1], rsum_both[:])
             o_sb = work.tile([P, D], F32, tag="o_sb", bufs=4, name="o_sb")
             nc.vector.tensor_scalar(
                 out=o_sb[:], in0=bank["o", j][:], scalar1=rinv[:, j : j + 1], scalar2=None, op0=ALU.mult
@@ -384,21 +412,28 @@ def tile_kanadjunction_pa_kernel(tc, source, target, k_right, WF_right, out):
         act_queue = []
         first = 0
         for size in PHASES:
-            act_queue.extend([("root", t) for t in range(first, first + size)])
-            act_queue.extend([("exp", t) for t in range(first, first + size)])
+            for t in range(first, first + size):
+                if t < SPLIT_ROOTS:
+                    act_queue.append(("root", t, 0, N // 2))
+                    act_queue.append(("root", t, N // 2, N))
+                else:
+                    act_queue.append(("root", t, 0, N))
+            act_queue.append(("shifts", first, first + size, 0))
+            act_queue.extend([("exp", t, 0, 0) for t in range(first, first + size)])
             first += size
         act_state = {"next": 0}
 
         def pump_act():
             while act_state["next"] < len(act_queue):
-                kind, t = act_queue[act_state["next"]]
+                kind, t, lo, hi = act_queue[act_state["next"]]
                 if kind == "root":
-                    if ("min", t) not in seen:
+                    if ("bank", NCH * t + hi // 512 - 1) not in seen:
                         break
-                    root(t)
-                    if t < 3:
-                        for s in range(4):
-                            square_t(4 * t + 4 + s)
+                    root(t, lo, hi)
+                elif kind == "shifts":
+                    if ("min", lo - 1) not in seen:
+                        break
+                    shifts(t, lo)
                 else:
                     if t >= E_BUFS and ("turned", t - E_BUFS) not in seen:
                         break
@@ -459,12 +494,13 @@ def tile_kanadjunction_pa_kernel(tc, source, target, k_right, WF_right, out):
                 )
                 if q == 1 and j >= 1:
                     post.append((None, lambda j=j: finish(j - 1), None))
-            post.append((None, lambda j=j: (e_quantise(j), weighted_sum(j)), None))
+                if q == 1 and j == BT - 1:
+                    post.append((None, lambda j=j: (e_quantise(j, 0, 4), weighted_sum(j, 0, 4)), None))
+            if j == BT - 1:
+                post.append((None, lambda j=j: (e_quantise(j, 4, NCH), weighted_sum(j, 4, NCH)), None))
+            else:
+                post.append((None, lambda j=j: (e_quantise(j, 0, NCH), weighted_sum(j, 0, NCH)), None))
         post.append((None, lambda: finish(BT - 1), None))
-
-        for i in range(4):
-            square_t(i)
-        norms_t(0, 4)
 
         def key_step(c):
             step(
@@ -472,7 +508,7 @@ def tile_kanadjunction_pa_kernel(tc, source, target, k_right, WF_right, out):
                 lambda c=c: k_transposes(c),
             )
             if c == 0:
-                step(lambda: t_out(0), lambda: t_transposes(0))
+                step(lambda: (t_out(0), [square_t(i) for i in range(4)], norms_t(0, 4)), lambda: t_transposes(0))
 
         for c in range(3):
             key_step(c)
@@ -481,13 +517,14 @@ def tile_kanadjunction_pa_kernel(tc, source, target, k_right, WF_right, out):
             if c + 3 < NCH:
                 key_step(c + 3)
             if c >= 1:
-                step(lambda c=c: clamp_min(c - 1))
+                step(lambda c=c: (clamp_min(c - 1), mark(("bank", c - 1))))
         step(
             lambda: (
                 [fold(8, s) for s in range(4)],
                 scores(8),
                 scores(9),
                 clamp_min(7),
+                mark(("bank", 7)),
                 scores(10),
                 row_min(0),
                 mark(("min", 0)),
@@ -497,9 +534,13 @@ def tile_kanadjunction_pa_kernel(tc, source, target, k_right, WF_right, out):
         taken = {"prep": 0, "post": 0}
         for x in range(NCH, BT * NCH):
             i, c = x // NCH, x % NCH
+            if 24 <= x < 28 or 32 <= x < 40:
+                step(lambda x=x: square_t(x - 20 if x < 28 else x - 24))
             if x == 30:
-                step(lambda: norms_t(4, BT))
-            step(lambda x=x: (clamp_min(x), scores(x + S_BANKS - 1)))
+                step(lambda: norms_t(4, 8))
+            if x == 41:
+                step(lambda: norms_t(8, BT))
+            step(lambda x=x: (clamp_min(x), mark(("bank", x)), scores(x + S_BANKS - 1)))
             if c == NCH - 1:
                 step(lambda i=i: (row_min(i), mark(("min", i))))
             share = PREP_PER_TILE[i] if i < len(PREP_PER_TILE) else 0

@@ -23,7 +23,7 @@ ZR_BUFS = 6
 E_BUFS = 4
 S_BANKS = 4
 X_BANKS = 3
-PHASES = (1, 2, 3, 3, 3, 4)
+PHASES = (1, 2, 3, 5, 5)
 LEAD = 6
 SPLIT_ROOTS = 3
 PREP_PER_TILE = (0, 13, 13, 13, 13, 4)

@@ -23,11 +23,11 @@ ZR_BUFS = 6
 E_BUFS = 4
 S_BANKS = 4
 X_BANKS = 3
-PHASES = (1, 2, 3, 5, 5)
+PHASES = (1, 2, 2, 3, 4, 4)
 LEAD = 6
 SPLIT_ROOTS = 3
-PREP_PER_TILE = (0, 13, 13, 13, 13, 4)
-POST_START = 44
+PREP_PER_TILE = (0, 10, 10, 10, 10, 10, 8)
+POST_START = 48
 POST_NUM, POST_DEN = 3, 4
 
 

@@ -28,7 +28,7 @@ LEAD = 6
 SPLIT_ROOTS = 3
 PREP_PER_TILE = (0, 10, 10, 10, 10, 10, 8)
 POST_START = 48
-POST_NUM, POST_DEN = 3, 4
+POST_NUM, POST_DEN = 7, 8
 
 
 def tile_kanadjunction_pa_kernel(tc, source, target, k_right, WF_right, out):
@@ -50,11 +50,11 @@ def tile_kanadjunction_pa_kernel(tc, source, target, k_right, WF_right, out):
 
         kT = keep.tile([P, 2, N], BF16, name="kT")
         tT = keep.tile([P, 2, B], BF16, name="tT")
-        kk_s = keep.tile([P, NT], F32, name="kk_s")
-        kk_v = keep.tile([P, NT], F32, name="kk_v")
+        kk = keep.tile([P, NT], F32, name="kk")
         tt = keep.tile([P, BT], F32, name="tt")
         negtt = keep.tile([P, BT], F32, name="negtt")
         tt256 = keep.tile([P, BT], F32, name="tt256")
+        zm8 = keep.tile([P, BT, NCH], F32, name="zm8")
         zmin = keep.tile([P, BT], F32, name="zmin")
         barg = keep.tile([P, BT], F32, name="barg")
         bexp = keep.tile([P, BT], F32, name="bexp")
@@ -63,7 +63,6 @@ def tile_kanadjunction_pa_kernel(tc, source, target, k_right, WF_right, out):
         rsum = keep.tile([P, BT], F32, name="rsum")
         rinv = keep.tile([P, BT], F32, name="rinv")
         junk = keep.tile([P, E], BF16, name="junk")
-        junk_v = keep.tile([P, E], F32, name="junk_v")
         fcodes = keep.tile([P, NCH, D], U32, name="fcodes", align_bytes=64)
         fscales = keep.tile([P, NCH, D], U8, name="fscales", align_bytes=64)
         wcodes = keep.tile([P, D], U32, name="wcodes", align_bytes=64)
@@ -109,29 +108,26 @@ def tile_kanadjunction_pa_kernel(tc, source, target, k_right, WF_right, out):
         def k_tile(m):
             return k_nat[m // 16][:, m % 16, :]
 
-        def vector_norm(rows, total):
-            nc.vector.scalar_tensor_tensor(
-                out=junk_v[:], in0=rows, scalar=1.0, in1=rows, op0=ALU.mult, op1=ALU.mult, accum_out=total
-            )
-
-        def square_t(i):
-            vector_norm(t_nat[:, i, :], tt[:, i : i + 1])
-
-        def kk_column(m):
-            return (kk_v if m % 4 == 3 else kk_s)[:, m : m + 1]
-
         def square_k(m):
-            if m % 4 == 3:
-                vector_norm(k_tile(m), kk_column(m))
-            else:
-                nc.scalar.activation(out=junk[:], in_=k_tile(m), func=ACTF.Square, accum_out=kk_column(m))
+            nc.scalar.activation(out=junk[:], in_=k_tile(m), func=ACTF.Square, accum_out=kk[:, m : m + 1])
 
         def norms_t(a, b):
-            nc.vector.tensor_scalar(
-                out=negtt[:, a:b], in0=tt[:, a:b], scalar1=-1.0, scalar2=None, op0=ALU.mult
+            sq = work.tile([P, 4, E], F32, tag="sq", bufs=1, name="sq")
+            rows = t_nat[:, a:b, :]
+            part = sq[:, 0 : b - a, :]
+            nc.gpsimd.tensor_tensor(out=part, in0=rows, in1=rows, op=ALU.mult)
+            width = E // 2
+            while width > 1:
+                nc.gpsimd.tensor_tensor(
+                    out=part[:, :, 0:width], in0=part[:, :, 0:width], in1=part[:, :, width : 2 * width], op=ALU.add
+                )
+                width //= 2
+            nc.gpsimd.tensor_tensor(out=tt[:, a:b], in0=part[:, :, 0], in1=part[:, :, 1], op=ALU.add)
+            nc.gpsimd.tensor_scalar(
+                out=negtt[:, a:b], in0=tt[:, a:b], scalar1=-1.0, scalar2=0.0, op0=ALU.mult, op1=ALU.add
             )
-            nc.vector.tensor_scalar(
-                out=tt256[:, a:b], in0=tt[:, a:b], scalar1=1.0 / 256.0, scalar2=None, op0=ALU.mult
+            nc.gpsimd.tensor_scalar(
+                out=tt256[:, a:b], in0=tt[:, a:b], scalar1=1.0 / 256.0, scalar2=0.0, op0=ALU.mult, op1=ALU.add
             )
 
         bank = {}
@@ -170,7 +166,6 @@ def tile_kanadjunction_pa_kernel(tc, source, target, k_right, WF_right, out):
             )
 
         zr = {}
-        zm8 = {}
 
         def fold(x, s):
             c = x % NCH
@@ -179,7 +174,7 @@ def tile_kanadjunction_pa_kernel(tc, source, target, k_right, WF_right, out):
             m = 4 * c + s
             nc.tensor.matmul(
                 bank["s", x][:, P * s : P * s + P],
-                lhsT=kk_column(m).to_broadcast([P, P]),
+                lhsT=kk[:, m : m + 1].to_broadcast([P, P]),
                 rhs=ident_f[:],
                 is_transpose=True,
                 start=(s == 0),
@@ -214,7 +209,6 @@ def tile_kanadjunction_pa_kernel(tc, source, target, k_right, WF_right, out):
             i, c = x // NCH, x % NCH
             if c == 0:
                 zr[i] = work.tile([P, N], F32, tag="zr", bufs=ZR_BUFS, name="zr")
-                zm8[i] = work.tile([P, NCH], F32, tag="zm8", bufs=2, name="zm8")
             nc.vector.tensor_scalar(
                 out=zr[i][:, 512 * c : 512 * c + 512],
                 in0=bank["s", x][:],
@@ -222,18 +216,18 @@ def tile_kanadjunction_pa_kernel(tc, source, target, k_right, WF_right, out):
                 scalar2=None,
                 op0=ALU.max,
                 op1=ALU.min,
-                accum_out=zm8[i][:, c : c + 1],
+                accum_out=zm8[:, i, c : c + 1],
             )
 
-        def row_min(i):
-            nc.vector.tensor_reduce(out=zmin[:, i : i + 1], in_=zm8[i][:], axis=AX.X, op=ALU.min)
+        def row_min(a, b):
+            nc.vector.tensor_reduce(out=zmin[:, a:b], in_=zm8[:, a:b, :], axis=AX.X, op=ALU.min)
 
         def root(i, lo, hi):
             nc.scalar.activation(
                 out=zr[i][:, lo:hi], in_=zr[i][:, lo:hi], func=ACTF.Sqrt, bias=tt[:, i : i + 1], scale=1.0
             )
 
-        def shifts(a, b):
+        def shift_squares(a, b):
             nc.vector.scalar_tensor_tensor(
                 out=barg[:, a:b],
                 in0=zmin[:, a:b],
@@ -242,6 +236,8 @@ def tile_kanadjunction_pa_kernel(tc, source, target, k_right, WF_right, out):
                 op0=ALU.mult,
                 op1=ALU.add,
             )
+
+        def shifts(a, b):
             nc.scalar.activation(out=bexp[:, a:b], in_=barg[:, a:b], func=ACTF.Sqrt)
 
         e_sb = {}
@@ -310,12 +306,14 @@ def tile_kanadjunction_pa_kernel(tc, source, target, k_right, WF_right, out):
                     stop=(g == NCH - 1),
                 )
 
-        def finish(j):
+        def invert_sum(j):
             if j < BT - 1:
                 nc.vector.reciprocal(rinv[:, j : j + 1], rsum[:, j : j + 1])
             else:
                 nc.vector.tensor_reduce(out=rsum_both[:], in_=rsum_last[:], axis=AX.X, op=ALU.add)
                 nc.vector.reciprocal(rinv[:, j : j + 1], rsum_both[:])
+
+        def finish(j):
             o_sb = work.tile([P, D], F32, tag="o_sb", bufs=4, name="o_sb")
             nc.vector.tensor_scalar(
                 out=o_sb[:], in0=bank["o", j][:], scalar1=rinv[:, j : j + 1], scalar2=None, op0=ALU.mult
@@ -431,7 +429,7 @@ def tile_kanadjunction_pa_kernel(tc, source, target, k_right, WF_right, out):
                         break
                     root(t, lo, hi)
                 elif kind == "shifts":
-                    if ("min", lo - 1) not in seen:
+                    if ("shift", lo) not in seen:
                         break
                     shifts(t, lo)
                 else:
@@ -492,14 +490,16 @@ def tile_kanadjunction_pa_kernel(tc, source, target, k_right, WF_right, out):
                         lambda j=j: j in e_sb,
                     )
                 )
-                if q == 1 and j >= 1:
+                if q == 0 and j >= 1:
+                    post.append((None, lambda j=j: (e_quantise(j - 1, 0, NCH), weighted_sum(j - 1, 0, NCH)), None))
+                if q == 1 and j < BT - 1:
+                    post.append((None, lambda j=j: invert_sum(j), None))
+                if q == 2 and j >= 1:
                     post.append((None, lambda j=j: finish(j - 1), None))
-                if q == 1 and j == BT - 1:
+                if q == 2 and j == BT - 1:
                     post.append((None, lambda j=j: (e_quantise(j, 0, 4), weighted_sum(j, 0, 4)), None))
-            if j == BT - 1:
-                post.append((None, lambda j=j: (e_quantise(j, 4, NCH), weighted_sum(j, 4, NCH)), None))
-            else:
-                post.append((None, lambda j=j: (e_quantise(j, 0, NCH), weighted_sum(j, 0, NCH)), None))
+        post.append((None, lambda: invert_sum(BT - 1), None))
+        post.append((None, lambda: (e_quantise(BT - 1, 4, NCH), weighted_sum(BT - 1, 4, NCH)), None))
         post.append((None, lambda: finish(BT - 1), None))
 
         def key_step(c):
@@ -508,7 +508,7 @@ def tile_kanadjunction_pa_kernel(tc, source, target, k_right, WF_right, out):
                 lambda c=c: k_transposes(c),
             )
             if c == 0:
-                step(lambda: (t_out(0), [square_t(i) for i in range(4)], norms_t(0, 4)), lambda: t_transposes(0))
+                step(lambda: (t_out(0), norms_t(0, 1), norms_t(1, 4)), lambda: t_transposes(0))
 
         for c in range(3):
             key_step(c)
@@ -526,23 +526,29 @@ def tile_kanadjunction_pa_kernel(tc, source, target, k_right, WF_right, out):
                 clamp_min(7),
                 mark(("bank", 7)),
                 scores(10),
-                row_min(0),
-                mark(("min", 0)),
             )
         )
+
+        phase_end = {}
+        first = 0
+        for size in PHASES:
+            phase_end[first + size] = first
+            first += size
+
+        def close_phase(a, b, part):
+            if part == 0:
+                step(lambda: row_min(a, b))
+            else:
+                step(lambda: (shift_squares(a, b), mark(("shift", b))))
 
         taken = {"prep": 0, "post": 0}
         for x in range(NCH, BT * NCH):
             i, c = x // NCH, x % NCH
-            if 24 <= x < 28 or 32 <= x < 40:
-                step(lambda x=x: square_t(x - 20 if x < 28 else x - 24))
-            if x == 30:
-                step(lambda: norms_t(4, 8))
-            if x == 41:
-                step(lambda: norms_t(8, BT))
+            if x in (8, 10, 12):
+                step(lambda x=x: norms_t(2 * x - 12, 2 * x - 8))
             step(lambda x=x: (clamp_min(x), mark(("bank", x)), scores(x + S_BANKS - 1)))
-            if c == NCH - 1:
-                step(lambda i=i: (row_min(i), mark(("min", i))))
+            if c < 2 and i in phase_end:
+                close_phase(phase_end[i], i, c)
             share = PREP_PER_TILE[i] if i < len(PREP_PER_TILE) else 0
             for r in range(share * (c + 1) // NCH - share * c // NCH):
                 if taken["prep"] < len(prep):
@@ -554,7 +560,11 @@ def tile_kanadjunction_pa_kernel(tc, source, target, k_right, WF_right, out):
                     steps.append(post[taken["post"]])
                     taken["post"] += 1
         steps.extend(prep[taken["prep"] :])
-        steps.extend(post[taken["post"] :])
+        rest = post[taken["post"] :]
+        for c in range(2):
+            close_phase(phase_end[BT], BT, c)
+            steps.append(rest.pop(0))
+        steps.extend(rest)
 
         fed = [idx for idx in range(len(steps)) if steps[idx][0] is not None]
         state = {"next": 0, "open": 0}

@@ -26,9 +26,11 @@ X_BANKS = 3
 PHASES = (1, 2, 2, 3, 4, 4)
 LEAD = 6
 SPLIT_ROOTS = 3
-PREP_PER_TILE = (0, 10, 10, 10, 10, 10, 8)
-POST_START = 48
-POST_NUM, POST_DEN = 7, 8
+RATE_NUM, RATE_DEN = 1, 1
+POST_LAG = 24
+POST_CAP = 2
+SUM_LAG = 3
+CODE_BUFS = 3
 
 
 def tile_kanadjunction_pa_kernel(tc, source, target, k_right, WF_right, out):
@@ -283,8 +285,8 @@ def tile_kanadjunction_pa_kernel(tc, source, target, k_right, WF_right, out):
 
         def e_quantise(j, g0, g1):
             if g0 == 0:
-                ecodes[j] = work.tile([P, NCH * P], U32, tag="ecodes", bufs=2, name="ecodes", align_bytes=64)
-                escales[j] = work.tile([P, NCH * P], U8, tag="escales", bufs=2, name="escales", align_bytes=64)
+                ecodes[j] = work.tile([P, NCH * P], U32, tag="ecodes", bufs=CODE_BUFS, name="ecodes", align_bytes=64)
+                escales[j] = work.tile([P, NCH * P], U8, tag="escales", bufs=CODE_BUFS, name="escales", align_bytes=64)
             nc.vector.quantize_mx(
                 out=ecodes[j][:, P * g0 : P * g1].bitcast(FP8X4),
                 scales=escales[j][:, P * g0 : P * g1],
@@ -480,27 +482,73 @@ def tile_kanadjunction_pa_kernel(tc, source, target, k_right, WF_right, out):
                 prep_item(lambda a=a: t_out(a), lambda a=a: t_transposes(a))
         prep_item(lambda: f_quantise(NCH - 1))
 
+        phase_end = {}
+        phase_of = {}
+        first = 0
+        for size in PHASES:
+            phase_end[first + size] = first
+            for j in range(first, first + size):
+                phase_of[j] = (first, first + size)
+            first += size
+
+        def earliest(j):
+            if j == BT:
+                return 2 * BT * NCH
+            a, b = phase_of[j]
+            return NCH * b + 4 * (j - a) + POST_LAG
+
         post = []
         for j in range(BT):
             for q in range(4):
                 post.append(
                     (
-                        lambda j=j, q=q: e_transposes(j, q),
-                        lambda j=j, q=q: (e_out(j, q), mark(("turned", j)) if q == 3 else None),
-                        lambda j=j: j in e_sb,
+                        lambda x, j=j: x >= earliest(j),
+                        False,
+                        (
+                            lambda j=j, q=q: e_transposes(j, q),
+                            lambda j=j, q=q: (e_out(j, q), mark(("turned", j)) if q == 3 else None),
+                            lambda j=j: j in e_sb,
+                        ),
                     )
                 )
                 if q == 0 and j >= 1:
-                    post.append((None, lambda j=j: (e_quantise(j - 1, 0, NCH), weighted_sum(j - 1, 0, NCH)), None))
+                    post.append((lambda x, j=j: has_room(j - 1), True, (None, lambda j=j: e_quantise(j - 1, 0, NCH), None)))
                 if q == 1 and j < BT - 1:
-                    post.append((None, lambda j=j: invert_sum(j), None))
-                if q == 2 and j >= 1:
-                    post.append((None, lambda j=j: finish(j - 1), None))
+                    post.append((lambda x: True, False, (None, lambda j=j: invert_sum(j), None)))
                 if q == 2 and j == BT - 1:
-                    post.append((None, lambda j=j: (e_quantise(j, 0, 4), weighted_sum(j, 0, 4)), None))
-        post.append((None, lambda: invert_sum(BT - 1), None))
-        post.append((None, lambda: (e_quantise(BT - 1, 4, NCH), weighted_sum(BT - 1, 4, NCH)), None))
-        post.append((None, lambda: finish(BT - 1), None))
+                    post.append((lambda x, j=j: has_room(j), True, (None, lambda j=j: e_quantise(j, 0, 4), None)))
+        post.append((lambda x: True, False, (None, lambda: invert_sum(BT - 1), None)))
+        post.append((lambda x: True, True, (None, lambda: e_quantise(BT - 1, 4, NCH), None)))
+
+        sums = [(j, 0, NCH) for j in range(BT - 1)] + [(BT - 1, 0, 4), (BT - 1, 4, NCH)]
+        done = {"prep": 0, "post": 0, "codes": 0, "sums": 0, "outputs": 0, "sum_at": 0}
+
+        def has_room(j):
+            return j < done["outputs"] + CODE_BUFS
+
+        def place_sum(x):
+            n = done["sums"]
+            if n and sums[n - 1][2] == NCH and done["outputs"] == sums[n - 1][0]:
+                if x >= done["sum_at"] + SUM_LAG:
+                    step(lambda j=done["outputs"]: finish(j))
+                    done["outputs"] += 1
+            elif n < done["codes"] and done["prep"] == len(prep):
+                step(lambda a=sums[n]: weighted_sum(*a))
+                done["sums"] += 1
+                done["sum_at"] = x
+
+        def place_piece(x):
+            n = done["post"]
+            if n < len(post) and post[n][0](x):
+                steps.append(post[n][2])
+                done["post"] += 1
+                done["codes"] += post[n][1]
+            elif done["prep"] < len(prep):
+                steps.append(prep[done["prep"]])
+                done["prep"] += 1
+            else:
+                return False
+            return True
 
         def key_step(c):
             step(
@@ -529,19 +577,13 @@ def tile_kanadjunction_pa_kernel(tc, source, target, k_right, WF_right, out):
             )
         )
 
-        phase_end = {}
-        first = 0
-        for size in PHASES:
-            phase_end[first + size] = first
-            first += size
-
         def close_phase(a, b, part):
             if part == 0:
                 step(lambda: row_min(a, b))
             else:
                 step(lambda: (shift_squares(a, b), mark(("shift", b))))
 
-        taken = {"prep": 0, "post": 0}
+        credit = 0
         for x in range(NCH, BT * NCH):
             i, c = x // NCH, x % NCH
             if x in (8, 10, 12):
@@ -549,22 +591,17 @@ def tile_kanadjunction_pa_kernel(tc, source, target, k_right, WF_right, out):
             step(lambda x=x: (clamp_min(x), mark(("bank", x)), scores(x + S_BANKS - 1)))
             if c < 2 and i in phase_end:
                 close_phase(phase_end[i], i, c)
-            share = PREP_PER_TILE[i] if i < len(PREP_PER_TILE) else 0
-            for r in range(share * (c + 1) // NCH - share * c // NCH):
-                if taken["prep"] < len(prep):
-                    steps.append(prep[taken["prep"]])
-                    taken["prep"] += 1
-            if x >= POST_START:
-                due = (x - POST_START + 1) * POST_NUM // POST_DEN
-                while taken["post"] < min(due, len(post)):
-                    steps.append(post[taken["post"]])
-                    taken["post"] += 1
-        steps.extend(prep[taken["prep"] :])
-        rest = post[taken["post"] :]
-        for c in range(2):
-            close_phase(phase_end[BT], BT, c)
-            steps.append(rest.pop(0))
-        steps.extend(rest)
+            place_sum(x)
+            credit = min(credit + RATE_NUM / RATE_DEN, POST_CAP)
+            while credit >= 1 and place_piece(x):
+                credit -= 1
+        x = BT * NCH
+        while done["outputs"] < BT:
+            if x < BT * NCH + 2:
+                close_phase(phase_end[BT], BT, x - BT * NCH)
+            place_piece(x if x < BT * NCH + 2 else earliest(BT))
+            place_sum(x)
+            x += 1
 
         fed = [idx for idx in range(len(steps)) if steps[idx][0] is not None]
         state = {"next": 0, "open": 0}

@@ -16,6 +16,7 @@ P = 128
 N, B, C, E, D = 4096, 2048, 512, 256, 256
 NT = N // P
 BT = B // P
+TT_PAD = 6
 NCH = N // 512
 FLOPS = 2 * (N * C * D + 2 * B * N * E)
 
@@ -24,12 +25,13 @@ E_BUFS = 4
 S_BANKS = 4
 X_BANKS = 3
 PHASES = (1, 2, 2, 3, 4, 4)
-LEAD = 6
+LEAD = 8
 SPLIT_ROOTS = 3
 RATE_NUM, RATE_DEN = 1, 1
 POST_LAG = 24
 POST_CAP = 2
 SUM_LAG = 3
+SCALE_AT = {11: (2, 4), 27: (4, 8), 48: (8, BT)}
 CODE_BUFS = 3
 
 
@@ -53,17 +55,18 @@ def tile_kanadjunction_pa_kernel(tc, source, target, k_right, WF_right, out):
         kT = keep.tile([P, 2, N], BF16, name="kT")
         tT = keep.tile([P, 2, B], BF16, name="tT")
         kk = keep.tile([P, NT], F32, name="kk")
-        tt = keep.tile([P, BT], F32, name="tt")
+        tt = keep.tile([P, TT_PAD + BT], F32, name="tt")
         negtt = keep.tile([P, BT], F32, name="negtt")
         tt256 = keep.tile([P, BT], F32, name="tt256")
         zm8 = keep.tile([P, BT, NCH], F32, name="zm8")
         zmin = keep.tile([P, BT], F32, name="zmin")
         barg = keep.tile([P, BT], F32, name="barg")
         bexp = keep.tile([P, BT], F32, name="bexp")
-        rsum_last = keep.tile([P, 2], F32, name="rsum_last")
+        rsum_last = keep.tile([P, 3], F32, name="rsum_last")
         rsum_both = keep.tile([P, 1], F32, name="rsum_both")
         rsum = keep.tile([P, BT], F32, name="rsum")
         rinv = keep.tile([P, BT], F32, name="rinv")
+        junk_v = keep.tile([P, E], F32, name="junk_v")
         junk = keep.tile([P, E], BF16, name="junk")
         fcodes = keep.tile([P, NCH, D], U32, name="fcodes", align_bytes=64)
         fscales = keep.tile([P, NCH, D], U8, name="fscales", align_bytes=64)
@@ -113,10 +116,10 @@ def tile_kanadjunction_pa_kernel(tc, source, target, k_right, WF_right, out):
         def square_k(m):
             nc.scalar.activation(out=junk[:], in_=k_tile(m), func=ACTF.Square, accum_out=kk[:, m : m + 1])
 
-        def norms_t(a, b):
+        def sums_of_squares(rows, total):
+            tiles = total.shape[1]
             sq = work.tile([P, 4, E], F32, tag="sq", bufs=1, name="sq")
-            rows = t_nat[:, a:b, :]
-            part = sq[:, 0 : b - a, :]
+            part = sq[:, 0:tiles, :]
             nc.gpsimd.tensor_tensor(out=part, in0=rows, in1=rows, op=ALU.mult)
             width = E // 2
             while width > 1:
@@ -124,13 +127,33 @@ def tile_kanadjunction_pa_kernel(tc, source, target, k_right, WF_right, out):
                     out=part[:, :, 0:width], in0=part[:, :, 0:width], in1=part[:, :, width : 2 * width], op=ALU.add
                 )
                 width //= 2
-            nc.gpsimd.tensor_tensor(out=tt[:, a:b], in0=part[:, :, 0], in1=part[:, :, 1], op=ALU.add)
-            nc.gpsimd.tensor_scalar(
-                out=negtt[:, a:b], in0=tt[:, a:b], scalar1=-1.0, scalar2=0.0, op0=ALU.mult, op1=ALU.add
+            nc.gpsimd.tensor_tensor(out=total, in0=part[:, :, 0], in1=part[:, :, 1], op=ALU.add)
+
+        def tt_columns(a, b):
+            pad = 0 if b <= 2 else TT_PAD
+            return tt[:, pad + a : pad + b]
+
+        def square_t(i):
+            nc.vector.scalar_tensor_tensor(
+                out=junk_v[:],
+                in0=t_nat[:, i, :],
+                scalar=1.0,
+                in1=t_nat[:, i, :],
+                op0=ALU.mult,
+                op1=ALU.mult,
+                accum_out=tt_columns(i, i + 1),
             )
-            nc.gpsimd.tensor_scalar(
-                out=tt256[:, a:b], in0=tt[:, a:b], scalar1=1.0 / 256.0, scalar2=0.0, op0=ALU.mult, op1=ALU.add
+
+        def scale_tt(a, b):
+            nc.vector.tensor_scalar(
+                out=negtt[:, a:b], in0=tt_columns(a, b), scalar1=-1.0, scalar2=None, op0=ALU.mult
             )
+            nc.vector.tensor_scalar(
+                out=tt256[:, a:b], in0=tt_columns(a, b), scalar1=1.0 / 256.0, scalar2=None, op0=ALU.mult
+            )
+
+        def norms_t(a, b):
+            sums_of_squares(t_nat[:, a:b, :], tt_columns(a, b))
 
         bank = {}
 
@@ -226,7 +249,7 @@ def tile_kanadjunction_pa_kernel(tc, source, target, k_right, WF_right, out):
 
         def root(i, lo, hi):
             nc.scalar.activation(
-                out=zr[i][:, lo:hi], in_=zr[i][:, lo:hi], func=ACTF.Sqrt, bias=tt[:, i : i + 1], scale=1.0
+                out=zr[i][:, lo:hi], in_=zr[i][:, lo:hi], func=ACTF.Sqrt, bias=tt_columns(i, i + 1), scale=1.0
             )
 
         def shift_squares(a, b):
@@ -249,7 +272,11 @@ def tile_kanadjunction_pa_kernel(tc, source, target, k_right, WF_right, out):
             if i < BT - 1:
                 pieces = [(0, N, rsum[:, i : i + 1])]
             else:
-                pieces = [(0, N // 2, rsum_last[:, 0:1]), (N // 2, N, rsum_last[:, 1:2])]
+                pieces = [
+                    (0, N // 2, rsum_last[:, 0:1]),
+                    (N // 2, 3 * N // 4, rsum_last[:, 1:2]),
+                    (3 * N // 4, N, rsum_last[:, 2:3]),
+                ]
             for lo, hi, total in pieces:
                 nc.scalar.activation(
                     out=e_sb[i][:, lo:hi],
@@ -497,6 +524,8 @@ def tile_kanadjunction_pa_kernel(tc, source, target, k_right, WF_right, out):
             a, b = phase_of[j]
             return NCH * b + 4 * (j - a) + POST_LAG
 
+        last_phase = phase_end[BT]
+        LAST_GROUPS = {4: 0, 6: 4, 8: 6}
         post = []
         for j in range(BT):
             for q in range(4):
@@ -511,16 +540,20 @@ def tile_kanadjunction_pa_kernel(tc, source, target, k_right, WF_right, out):
                         ),
                     )
                 )
-                if q == 0 and j >= 1:
+                if q == 0 and 1 <= j <= last_phase:
                     post.append((lambda x, j=j: has_room(j - 1), True, (None, lambda j=j: e_quantise(j - 1, 0, NCH), None)))
-                if q == 1 and j < BT - 1:
+                if q == 1 and j < last_phase:
                     post.append((lambda x: True, False, (None, lambda j=j: invert_sum(j), None)))
-                if q == 2 and j == BT - 1:
-                    post.append((lambda x, j=j: has_room(j), True, (None, lambda j=j: e_quantise(j, 0, 4), None)))
-        post.append((lambda x: True, False, (None, lambda: invert_sum(BT - 1), None)))
-        post.append((lambda x: True, True, (None, lambda: e_quantise(BT - 1, 4, NCH), None)))
+                if j == BT - 1 and q >= 1:
+                    g1 = 2 * q + 2
+                    if q == 3:
+                        post.append((lambda x: True, False, (None, lambda: invert_sum(BT - 1), None)))
+                    post.append((lambda x: True, True, (None, lambda g1=g1: e_quantise(BT - 1, LAST_GROUPS[g1], g1), None)))
+                elif j >= last_phase and q == 3:
+                    post.append((lambda x: True, False, (None, lambda j=j: invert_sum(j), None)))
+                    post.append((lambda x, j=j: has_room(j), True, (None, lambda j=j: e_quantise(j, 0, NCH), None)))
 
-        sums = [(j, 0, NCH) for j in range(BT - 1)] + [(BT - 1, 0, 4), (BT - 1, 4, NCH)]
+        sums = [(j, 0, NCH) for j in range(BT - 1)] + [(BT - 1, g0, g1) for g1, g0 in LAST_GROUPS.items()]
         done = {"prep": 0, "post": 0, "codes": 0, "sums": 0, "outputs": 0, "sum_at": 0}
 
         def has_room(j):
@@ -552,12 +585,16 @@ def tile_kanadjunction_pa_kernel(tc, source, target, k_right, WF_right, out):
 
         def key_step(c):
             step(
-                lambda c=c: (k_out(c), [square_k(4 * c + s) for s in range(4)]),
+                lambda c=c: (
+                    k_out(c),
+                    [square_k(4 * c + s) for s in range(4)],
+                ),
                 lambda c=c: k_transposes(c),
             )
             if c == 0:
-                step(lambda: (t_out(0), norms_t(0, 1), norms_t(1, 4)), lambda: t_transposes(0))
+                step(lambda: (t_out(0), square_t(0), square_t(1), scale_tt(0, 2)), lambda: t_transposes(0))
 
+        step(lambda: [norms_t(a, b) for a, b in ((2, 4), (4, 8), (8, 12), (12, BT))])
         for c in range(3):
             key_step(c)
         for c in range(NCH):
@@ -569,11 +606,10 @@ def tile_kanadjunction_pa_kernel(tc, source, target, k_right, WF_right, out):
         step(
             lambda: (
                 [fold(8, s) for s in range(4)],
-                scores(8),
-                scores(9),
+                [scores(x) for x in range(NCH, NCH + S_BANKS - 2)],
                 clamp_min(7),
                 mark(("bank", 7)),
-                scores(10),
+                scores(NCH + S_BANKS - 2),
             )
         )
 
@@ -586,8 +622,8 @@ def tile_kanadjunction_pa_kernel(tc, source, target, k_right, WF_right, out):
         credit = 0
         for x in range(NCH, BT * NCH):
             i, c = x // NCH, x % NCH
-            if x in (8, 10, 12):
-                step(lambda x=x: norms_t(2 * x - 12, 2 * x - 8))
+            if x in SCALE_AT:
+                step(lambda x=x: scale_tt(*SCALE_AT[x]))
             step(lambda x=x: (clamp_min(x), mark(("bank", x)), scores(x + S_BANKS - 1)))
             if c < 2 and i in phase_end:
                 close_phase(phase_end[i], i, c)

@@ -21,18 +21,22 @@ NCH = N // 512
 FLOPS = 2 * (N * C * D + 2 * B * N * E)
 
 ZR_BUFS = 6
-E_BUFS = 4
+E_BUFS = 6
 S_BANKS = 4
+SRC_BUFS = 2
 X_BANKS = 3
-PHASES = (1, 2, 2, 3, 4, 4)
+PHASES = (1, 3, 4, 4, 4)
 LEAD = 8
 SPLIT_ROOTS = 3
-RATE_NUM, RATE_DEN = 1, 1
-POST_LAG = 24
+R0 = 0.5
+R1 = 1
+X1 = 40
+POST_LAG = 20
 POST_CAP = 2
-SUM_LAG = 3
+SUM_LAG = 4
 SCALE_AT = {11: (2, 4), 27: (4, 8), 48: (8, BT)}
 CODE_BUFS = 3
+LATE = ((BT - 1, 2), (BT - 1, 3))
 
 
 def tile_kanadjunction_pa_kernel(tc, source, target, k_right, WF_right, out):
@@ -101,14 +105,11 @@ def tile_kanadjunction_pa_kernel(tc, source, target, k_right, WF_right, out):
         src = {}
 
         def load_src(g):
-            src[g] = work.tile([P, 4, C], BF16, tag="src", bufs=2, name="src")
-            nc.sync.dma_start(
-                out=src[g][:].rearrange("p (u e) c -> p u (e c)", u=2),
-                in_=s_view[:, 2 * g : 2 * g + 2, :],
-            )
+            src[g] = work.tile([P, 2, C], BF16, tag="src", bufs=SRC_BUFS, name="src")
+            nc.sync.dma_start(out=src[g][:].rearrange("p e c -> p (e c)"), in_=s_view[:, g, :])
 
-        load_src(0)
-        load_src(1)
+        for g in range(SRC_BUFS):
+            load_src(g)
 
         def k_tile(m):
             return k_nat[m // 16][:, m % 16, :]
@@ -118,7 +119,7 @@ def tile_kanadjunction_pa_kernel(tc, source, target, k_right, WF_right, out):
 
         def sums_of_squares(rows, total):
             tiles = total.shape[1]
-            sq = work.tile([P, 4, E], F32, tag="sq", bufs=1, name="sq")
+            sq = work.tile([P, 2, E], F32, tag="sq", bufs=1, name="sq")
             part = sq[:, 0:tiles, :]
             nc.gpsimd.tensor_tensor(out=part, in0=rows, in1=rows, op=ALU.mult)
             width = E // 2
@@ -305,7 +306,8 @@ def tile_kanadjunction_pa_kernel(tc, source, target, k_right, WF_right, out):
                 egrp[j] = work.tile(
                     [P, NCH, P, 4], BF16, tag="egrp", bufs=2, name="egrp", align_bytes=64
                 )
-            nc.vector.tensor_copy(
+            copy = nc.scalar.copy if (j, q) in LATE else nc.vector.tensor_copy
+            copy(
                 out=egrp[j][:].bitcast(F32)[:, 2 * q : 2 * q + 2, :, :],
                 in_=bank["e", j, q][:].rearrange("p g u b -> p g b u"),
             )
@@ -343,7 +345,7 @@ def tile_kanadjunction_pa_kernel(tc, source, target, k_right, WF_right, out):
                 nc.vector.reciprocal(rinv[:, j : j + 1], rsum_both[:])
 
         def finish(j):
-            o_sb = work.tile([P, D], F32, tag="o_sb", bufs=4, name="o_sb")
+            o_sb = work.tile([P, D], F32, tag="o_sb", bufs=2, name="o_sb")
             nc.vector.tensor_scalar(
                 out=o_sb[:], in0=bank["o", j][:], scalar1=rinv[:, j : j + 1], scalar2=None, op0=ALU.mult
             )
@@ -378,22 +380,20 @@ def tile_kanadjunction_pa_kernel(tc, source, target, k_right, WF_right, out):
         def s_transposes(g, half):
             xs = psum.tile([P, 2, 2, P], F32, tag="x", bufs=X_BANKS, name="xs")
             bank["src", g, half] = xs
-            words = src[g][:].bitcast(F32)
+            words = src[2 * g + half][:].bitcast(F32)
             for tl in range(2):
                 for u in range(2):
-                    nc.tensor.transpose(
-                        xs[:, tl, u, :], words[:, 2 * half + tl, P * u : P * u + P], ident_f[:]
-                    )
+                    nc.tensor.transpose(xs[:, tl, u, :], words[:, tl, P * u : P * u + P], ident_f[:])
 
         def s_out(g, half):
             if half == 0:
-                sgrp[g] = work.tile([P, 4, P, 4], BF16, tag="sgrp", bufs=2, name="sgrp", align_bytes=64)
+                sgrp[g] = work.tile([P, 4, P, 4], BF16, tag="sgrp", bufs=1, name="sgrp", align_bytes=64)
             nc.vector.tensor_copy(
                 out=sgrp[g][:].bitcast(F32)[:, 2 * half : 2 * half + 2, :, :],
                 in_=bank["src", g, half][:].rearrange("p t u n -> p t n u"),
             )
-            if half == 1 and g + 2 < NCH:
-                load_src(g + 2)
+            if 2 * g + half + SRC_BUFS < 2 * NCH:
+                load_src(2 * g + half + SRC_BUFS)
 
         def s_quantise(g):
             scodes[g] = work.tile([P, 4 * P], U32, tag="scodes", bufs=2, name="scodes", align_bytes=64)
@@ -420,7 +420,7 @@ def tile_kanadjunction_pa_kernel(tc, source, target, k_right, WF_right, out):
 
         def f_out(g, dh):
             if dh == 0:
-                fgrp[g] = work.tile([P, D, 4], BF16, tag="fgrp", bufs=2, name="fgrp", align_bytes=64)
+                fgrp[g] = work.tile([P, D, 4], BF16, tag="fgrp", bufs=1, name="fgrp", align_bytes=64)
             nc.vector.tensor_copy(
                 out=fgrp[g][:, P * dh : P * dh + P, :],
                 in_=bank["f", g, dh][:].rearrange("p t d -> p d t"),
@@ -483,10 +483,11 @@ def tile_kanadjunction_pa_kernel(tc, source, target, k_right, WF_right, out):
                 prep_item(
                     lambda g=g, half=half: s_out(g, half),
                     lambda g=g, half=half: s_transposes(g, half),
-                    lambda g=g: g in src,
+                    lambda g=g, half=half: 2 * g + half in src,
                 )
 
-        prep_item(lambda: t_out(1), lambda: t_transposes(1))
+        for a in range(1, BT // 4):
+            prep_item(lambda a=a: t_out(a), lambda a=a: t_transposes(a))
         prep_item(w_out, w_transposes)
         source_items(0)
         prep_item(w_quantise)
@@ -504,9 +505,6 @@ def tile_kanadjunction_pa_kernel(tc, source, target, k_right, WF_right, out):
                     lambda g=g, dh=dh: f_matmuls(g, dh),
                     lambda g=g: g in scodes,
                 )
-            if g in (1, 3):
-                a = (g + 3) // 2
-                prep_item(lambda a=a: t_out(a), lambda a=a: t_transposes(a))
         prep_item(lambda: f_quantise(NCH - 1))
 
         phase_end = {}
@@ -572,7 +570,7 @@ def tile_kanadjunction_pa_kernel(tc, source, target, k_right, WF_right, out):
 
         def place_piece(x):
             n = done["post"]
-            if n < len(post) and post[n][0](x):
+            if n < len(post) and post[n][0](x if x < BT * NCH + 2 else earliest(BT)):
                 steps.append(post[n][2])
                 done["post"] += 1
                 done["codes"] += post[n][1]
@@ -594,9 +592,9 @@ def tile_kanadjunction_pa_kernel(tc, source, target, k_right, WF_right, out):
             if c == 0:
                 step(lambda: (t_out(0), square_t(0), square_t(1), scale_tt(0, 2)), lambda: t_transposes(0))
 
-        step(lambda: [norms_t(a, b) for a, b in ((2, 4), (4, 8), (8, 12), (12, BT))])
         for c in range(3):
             key_step(c)
+        step(lambda: [norms_t(a, a + 2) for a in range(2, BT, 2)])
         for c in range(NCH):
             step(lambda c=c: whole_bank(c))
             if c + 3 < NCH:
@@ -628,14 +626,14 @@ def tile_kanadjunction_pa_kernel(tc, source, target, k_right, WF_right, out):
             if c < 2 and i in phase_end:
                 close_phase(phase_end[i], i, c)
             place_sum(x)
-            credit = min(credit + RATE_NUM / RATE_DEN, POST_CAP)
+            credit = min(credit + (R0 if x < X1 else R1), POST_CAP)
             while credit >= 1 and place_piece(x):
                 credit -= 1
         x = BT * NCH
         while done["outputs"] < BT:
             if x < BT * NCH + 2:
                 close_phase(phase_end[BT], BT, x - BT * NCH)
-            place_piece(x if x < BT * NCH + 2 else earliest(BT))
+            place_piece(x)
             place_sum(x)
             x += 1
 

@@ -71,13 +71,11 @@ def tile_kanadjunction_pa_kernel(tc, source, target, k_right, WF_right, out):
         rsum = keep.tile([P, BT], F32, name="rsum")
         rinv = keep.tile([P, BT], F32, name="rinv")
         junk_v = keep.tile([P, E], F32, name="junk_v")
-        junk = keep.tile([P, E], BF16, name="junk")
+        junk = keep.tile([P, 4, E], BF16, name="junk")
         fcodes = keep.tile([P, NCH, D], U32, name="fcodes", align_bytes=64)
         fscales = keep.tile([P, NCH, D], U8, name="fscales", align_bytes=64)
         wcodes = keep.tile([P, D], U32, name="wcodes", align_bytes=64)
         wscales = keep.tile([P, D], U8, name="wscales", align_bytes=64)
-        wf_nat = keep.tile([P, 2, C], BF16, name="wf_nat")
-        wgrp = keep.tile([P, D, 4], BF16, name="wgrp", align_bytes=64)
 
         k_view = k_right.rearrange("(m p) j -> p m j", p=P)
         t_view = target.rearrange("(i p) j -> p i j", p=P)
@@ -100,7 +98,9 @@ def tile_kanadjunction_pa_kernel(tc, source, target, k_right, WF_right, out):
         load_k(2)
         load_k(3)
         nc.sync.dma_start(out=t_nat[:, 4:BT, :], in_=t_view[:, 4:BT, :])
+        wf_nat = work.tile([P, 2, C], BF16, tag="src", bufs=SRC_BUFS, name="wf_nat")
         nc.sync.dma_start(out=wf_nat[:], in_=WF_right.rearrange("(h p) c -> p h c", p=P))
+        wgrp = work.tile([P, D, 4], BF16, tag="fgrp", bufs=1, name="wgrp", align_bytes=64)
 
         src = {}
 
@@ -108,14 +108,14 @@ def tile_kanadjunction_pa_kernel(tc, source, target, k_right, WF_right, out):
             src[g] = work.tile([P, 2, C], BF16, tag="src", bufs=SRC_BUFS, name="src")
             nc.sync.dma_start(out=src[g][:].rearrange("p e c -> p (e c)"), in_=s_view[:, g, :])
 
-        for g in range(SRC_BUFS):
+        for g in range(SRC_BUFS - 1):
             load_src(g)
 
         def k_tile(m):
             return k_nat[m // 16][:, m % 16, :]
 
         def square_k(m):
-            nc.scalar.activation(out=junk[:], in_=k_tile(m), func=ACTF.Square, accum_out=kk[:, m : m + 1])
+            nc.scalar.activation(out=junk[:, m % 4, :], in_=k_tile(m), func=ACTF.Square, accum_out=kk[:, m : m + 1])
 
         def sums_of_squares(rows, total):
             tiles = total.shape[1]
@@ -369,6 +369,7 @@ def tile_kanadjunction_pa_kernel(tc, source, target, k_right, WF_right, out):
                 out=wgrp[:].bitcast(F32).rearrange("p (h d) u -> p h d u", h=2),
                 in_=bank["w"][:].rearrange("p h u d -> p h d u"),
             )
+            load_src(SRC_BUFS - 1)
 
         def w_quantise():
             nc.vector.quantize_mx(

@@ -28,15 +28,14 @@ X_BANKS = 3
 PHASES = (1, 3, 4, 4, 4)
 LEAD = 8
 SPLIT_ROOTS = 3
-R0 = 0.5
+R0 = 0.75
 R1 = 1
-X1 = 40
+X1 = 48
 POST_LAG = 20
 POST_CAP = 2
 SUM_LAG = 4
-SCALE_AT = {11: (2, 4), 27: (4, 8), 48: (8, BT)}
 CODE_BUFS = 3
-LATE = ((BT - 1, 2), (BT - 1, 3))
+LATE = tuple((BT - 1, q) for q in range(4))
 
 
 def tile_kanadjunction_pa_kernel(tc, source, target, k_right, WF_right, out):
@@ -60,17 +59,16 @@ def tile_kanadjunction_pa_kernel(tc, source, target, k_right, WF_right, out):
         tT = keep.tile([P, 2, B], BF16, name="tT")
         kk = keep.tile([P, NT], F32, name="kk")
         tt = keep.tile([P, TT_PAD + BT], F32, name="tt")
-        negtt = keep.tile([P, BT], F32, name="negtt")
-        tt256 = keep.tile([P, BT], F32, name="tt256")
+        negtt = keep.tile([P, TT_PAD + BT], F32, name="negtt")
+        tt256 = keep.tile([P, TT_PAD + BT], F32, name="tt256")
         zm8 = keep.tile([P, BT, NCH], F32, name="zm8")
         zmin = keep.tile([P, BT], F32, name="zmin")
-        barg = keep.tile([P, BT], F32, name="barg")
         bexp = keep.tile([P, BT], F32, name="bexp")
         rsum_last = keep.tile([P, 3], F32, name="rsum_last")
         rsum_both = keep.tile([P, 1], F32, name="rsum_both")
         rsum = keep.tile([P, BT], F32, name="rsum")
         rinv = keep.tile([P, BT], F32, name="rinv")
-        junk_v = keep.tile([P, E], F32, name="junk_v")
+        junk_v = keep.tile([P, 2, E], F32, name="junk_v")
         junk = keep.tile([P, 4, E], BF16, name="junk")
         fcodes = keep.tile([P, NCH, D], U32, name="fcodes", align_bytes=64)
         fscales = keep.tile([P, NCH, D], U8, name="fscales", align_bytes=64)
@@ -86,17 +84,14 @@ def tile_kanadjunction_pa_kernel(tc, source, target, k_right, WF_right, out):
         ]
         t_nat = work.tile([P, BT, E], BF16, tag="e", bufs=E_BUFS, name="t_nat")
 
-        def load_k(q):
-            nc.sync.dma_start(
-                out=k_nat[q // 2][:, 8 * (q % 2) : 8 * (q % 2) + 8, :],
-                in_=k_view[:, 8 * q : 8 * q + 8, :],
-            )
+        def load_k(a, b):
+            lo = a % (NT // 2)
+            nc.sync.dma_start(out=k_nat[a // (NT // 2)][:, lo : lo + b - a, :], in_=k_view[:, a:b, :])
 
-        load_k(0)
+        load_k(0, 4)
         nc.sync.dma_start(out=t_nat[:, 0:4, :], in_=t_view[:, 0:4, :])
-        load_k(1)
-        load_k(2)
-        load_k(3)
+        for a, b in ((4, 8), (8, 16), (16, 24), (24, 32)):
+            load_k(a, b)
         nc.sync.dma_start(out=t_nat[:, 4:BT, :], in_=t_view[:, 4:BT, :])
         wf_nat = work.tile([P, 2, C], BF16, tag="src", bufs=SRC_BUFS, name="wf_nat")
         nc.sync.dma_start(out=wf_nat[:], in_=WF_right.rearrange("(h p) c -> p h c", p=P))
@@ -130,31 +125,35 @@ def tile_kanadjunction_pa_kernel(tc, source, target, k_right, WF_right, out):
                 width //= 2
             nc.gpsimd.tensor_tensor(out=total, in0=part[:, :, 0], in1=part[:, :, 1], op=ALU.add)
 
-        def tt_columns(a, b):
+        def columns(norms, a, b):
             pad = 0 if b <= 2 else TT_PAD
-            return tt[:, pad + a : pad + b]
+            return norms[:, pad + a : pad + b]
 
         def square_t(i):
             nc.vector.scalar_tensor_tensor(
-                out=junk_v[:],
+                out=junk_v[:, i, :],
                 in0=t_nat[:, i, :],
                 scalar=1.0,
                 in1=t_nat[:, i, :],
                 op0=ALU.mult,
                 op1=ALU.mult,
-                accum_out=tt_columns(i, i + 1),
+                accum_out=columns(tt, i, i + 1),
             )
 
-        def scale_tt(a, b):
-            nc.vector.tensor_scalar(
-                out=negtt[:, a:b], in0=tt_columns(a, b), scalar1=-1.0, scalar2=None, op0=ALU.mult
-            )
-            nc.vector.tensor_scalar(
-                out=tt256[:, a:b], in0=tt_columns(a, b), scalar1=1.0 / 256.0, scalar2=None, op0=ALU.mult
-            )
+        def scale_tt(engine, a, b):
+            for out, factor in ((negtt, -1.0), (tt256, 1.0 / 256.0)):
+                engine.tensor_scalar(
+                    out=columns(out, a, b),
+                    in0=columns(tt, a, b),
+                    scalar1=factor,
+                    scalar2=0.0,
+                    op0=ALU.mult,
+                    op1=ALU.add,
+                )
 
         def norms_t(a, b):
-            sums_of_squares(t_nat[:, a:b, :], tt_columns(a, b))
+            sums_of_squares(t_nat[:, a:b, :], columns(tt, a, b))
+            scale_tt(nc.gpsimd, a, b)
 
         bank = {}
 
@@ -238,7 +237,7 @@ def tile_kanadjunction_pa_kernel(tc, source, target, k_right, WF_right, out):
             nc.vector.tensor_scalar(
                 out=zr[i][:, 512 * c : 512 * c + 512],
                 in0=bank["s", x][:],
-                scalar1=negtt[:, i : i + 1],
+                scalar1=columns(negtt, i, i + 1),
                 scalar2=None,
                 op0=ALU.max,
                 op1=ALU.min,
@@ -250,21 +249,18 @@ def tile_kanadjunction_pa_kernel(tc, source, target, k_right, WF_right, out):
 
         def root(i, lo, hi):
             nc.scalar.activation(
-                out=zr[i][:, lo:hi], in_=zr[i][:, lo:hi], func=ACTF.Sqrt, bias=tt_columns(i, i + 1), scale=1.0
-            )
-
-        def shift_squares(a, b):
-            nc.vector.scalar_tensor_tensor(
-                out=barg[:, a:b],
-                in0=zmin[:, a:b],
-                scalar=1.0 / 256.0,
-                in1=tt256[:, a:b],
-                op0=ALU.mult,
-                op1=ALU.add,
+                out=zr[i][:, lo:hi], in_=zr[i][:, lo:hi], func=ACTF.Sqrt, bias=columns(tt, i, i + 1), scale=1.0
             )
 
         def shifts(a, b):
-            nc.scalar.activation(out=bexp[:, a:b], in_=barg[:, a:b], func=ACTF.Sqrt)
+            for i in range(a, b):
+                nc.scalar.activation(
+                    out=bexp[:, i : i + 1],
+                    in_=zmin[:, i : i + 1],
+                    func=ACTF.Sqrt,
+                    bias=columns(tt256, i, i + 1),
+                    scale=1.0 / 256.0,
+                )
 
         e_sb = {}
 
@@ -571,7 +567,7 @@ def tile_kanadjunction_pa_kernel(tc, source, target, k_right, WF_right, out):
 
         def place_piece(x):
             n = done["post"]
-            if n < len(post) and post[n][0](x if x < BT * NCH + 2 else earliest(BT)):
+            if n < len(post) and post[n][0](x if x < BT * NCH + 1 else earliest(BT)):
                 steps.append(post[n][2])
                 done["post"] += 1
                 done["codes"] += post[n][1]
@@ -591,7 +587,9 @@ def tile_kanadjunction_pa_kernel(tc, source, target, k_right, WF_right, out):
                 lambda c=c: k_transposes(c),
             )
             if c == 0:
-                step(lambda: (t_out(0), square_t(0), square_t(1), scale_tt(0, 2)), lambda: t_transposes(0))
+                step(lambda: (t_out(0), square_t(0), square_t(1)), lambda: t_transposes(0))
+            if c == 1:
+                step(lambda: scale_tt(nc.vector, 0, 2))
 
         for c in range(3):
             key_step(c)
@@ -612,29 +610,24 @@ def tile_kanadjunction_pa_kernel(tc, source, target, k_right, WF_right, out):
             )
         )
 
-        def close_phase(a, b, part):
-            if part == 0:
-                step(lambda: row_min(a, b))
-            else:
-                step(lambda: (shift_squares(a, b), mark(("shift", b))))
+        def close_phase(a, b):
+            step(lambda: (row_min(a, b), mark(("shift", b))))
 
         credit = 0
         for x in range(NCH, BT * NCH):
             i, c = x // NCH, x % NCH
-            if x in SCALE_AT:
-                step(lambda x=x: scale_tt(*SCALE_AT[x]))
             step(lambda x=x: (clamp_min(x), mark(("bank", x)), scores(x + S_BANKS - 1)))
-            if c < 2 and i in phase_end:
-                close_phase(phase_end[i], i, c)
+            if c == 0 and i in phase_end:
+                close_phase(phase_end[i], i)
             place_sum(x)
             credit = min(credit + (R0 if x < X1 else R1), POST_CAP)
             while credit >= 1 and place_piece(x):
                 credit -= 1
         x = BT * NCH
         while done["outputs"] < BT:
-            if x < BT * NCH + 2:
-                close_phase(phase_end[BT], BT, x - BT * NCH)
             place_piece(x)
+            if x == BT * NCH:
+                close_phase(phase_end[BT], BT)
             place_sum(x)
             x += 1
 

@@ -31,10 +31,14 @@ SPLIT_ROOTS = 3
 R0 = 0.75
 R1 = 1
 X1 = 48
-POST_LAG = 20
-POST_CAP = 2
+POST_LAG = 24
+POST_CAP = 1.5
 SUM_LAG = 4
 CODE_BUFS = 3
+OWN_FROM = BT - 1
+HOLD = 6
+SQ_AT = 0
+NORMS_AT = tuple(range(8, 36, 4))
 LATE = tuple((BT - 1, q) for q in range(4))
 
 
@@ -65,7 +69,6 @@ def tile_kanadjunction_pa_kernel(tc, source, target, k_right, WF_right, out):
         zmin = keep.tile([P, BT], F32, name="zmin")
         bexp = keep.tile([P, BT], F32, name="bexp")
         rsum_last = keep.tile([P, 3], F32, name="rsum_last")
-        rsum_both = keep.tile([P, 1], F32, name="rsum_both")
         rsum = keep.tile([P, BT], F32, name="rsum")
         rinv = keep.tile([P, BT], F32, name="rinv")
         junk_v = keep.tile([P, 2, E], F32, name="junk_v")
@@ -109,21 +112,11 @@ def tile_kanadjunction_pa_kernel(tc, source, target, k_right, WF_right, out):
         def k_tile(m):
             return k_nat[m // 16][:, m % 16, :]
 
-        def square_k(m):
-            nc.scalar.activation(out=junk[:, m % 4, :], in_=k_tile(m), func=ACTF.Square, accum_out=kk[:, m : m + 1])
+        def square_rows(rows, total, row):
+            nc.scalar.activation(out=junk[:, row % 4, :], in_=rows, func=ACTF.Square, accum_out=total)
 
-        def sums_of_squares(rows, total):
-            tiles = total.shape[1]
-            sq = work.tile([P, 2, E], F32, tag="sq", bufs=1, name="sq")
-            part = sq[:, 0:tiles, :]
-            nc.gpsimd.tensor_tensor(out=part, in0=rows, in1=rows, op=ALU.mult)
-            width = E // 2
-            while width > 1:
-                nc.gpsimd.tensor_tensor(
-                    out=part[:, :, 0:width], in0=part[:, :, 0:width], in1=part[:, :, width : 2 * width], op=ALU.add
-                )
-                width //= 2
-            nc.gpsimd.tensor_tensor(out=total, in0=part[:, :, 0], in1=part[:, :, 1], op=ALU.add)
+        def square_k(m):
+            square_rows(k_tile(m), kk[:, m : m + 1], m)
 
         def columns(norms, a, b):
             pad = 0 if b <= 2 else TT_PAD
@@ -152,7 +145,8 @@ def tile_kanadjunction_pa_kernel(tc, source, target, k_right, WF_right, out):
                 )
 
         def norms_t(a, b):
-            sums_of_squares(t_nat[:, a:b, :], columns(tt, a, b))
+            for i in range(a, b):
+                square_rows(t_nat[:, i, :], columns(tt, i, i + 1), i)
             scale_tt(nc.gpsimd, a, b)
 
         bank = {}
@@ -320,7 +314,10 @@ def tile_kanadjunction_pa_kernel(tc, source, target, k_right, WF_right, out):
 
         def weighted_sum(j, g0, g1):
             if g0 == 0:
-                bank["o", j] = psum.tile([P, D], F32, tag="o", bufs=1, name="po")
+                if j < OWN_FROM:
+                    bank["o", j] = psum.tile([P, D], F32, tag="o", bufs=1, name="po")
+                else:
+                    bank["o", j] = psum.tile([P, D], F32, tag="s", bufs=S_BANKS, name="po_last")
             po = bank["o", j]
             for g in range(g0, g1):
                 nc.tensor.matmul_mx(
@@ -333,12 +330,11 @@ def tile_kanadjunction_pa_kernel(tc, source, target, k_right, WF_right, out):
                     stop=(g == NCH - 1),
                 )
 
+        def add_last_sums():
+            nc.vector.tensor_reduce(out=rsum[:, BT - 1 : BT], in_=rsum_last[:], axis=AX.X, op=ALU.add)
+
         def invert_sum(j):
-            if j < BT - 1:
-                nc.vector.reciprocal(rinv[:, j : j + 1], rsum[:, j : j + 1])
-            else:
-                nc.vector.tensor_reduce(out=rsum_both[:], in_=rsum_last[:], axis=AX.X, op=ALU.add)
-                nc.vector.reciprocal(rinv[:, j : j + 1], rsum_both[:])
+            nc.vector.reciprocal(rinv[:, j : j + 1], rsum[:, j : j + 1])
 
         def finish(j):
             o_sb = work.tile([P, D], F32, tag="o_sb", bufs=2, name="o_sb")
@@ -541,29 +537,36 @@ def tile_kanadjunction_pa_kernel(tc, source, target, k_right, WF_right, out):
                     post.append((lambda x: True, False, (None, lambda j=j: invert_sum(j), None)))
                 if j == BT - 1 and q >= 1:
                     g1 = 2 * q + 2
-                    if q == 3:
-                        post.append((lambda x: True, False, (None, lambda: invert_sum(BT - 1), None)))
+                    if q == 2:
+                        post.append((lambda x: True, False, (None, add_last_sums, None)))
                     post.append((lambda x: True, True, (None, lambda g1=g1: e_quantise(BT - 1, LAST_GROUPS[g1], g1), None)))
+                    if q == 2:
+                        post.append((lambda x: True, False, (None, lambda: invert_sum(BT - 1), None)))
                 elif j >= last_phase and q == 3:
                     post.append((lambda x: True, False, (None, lambda j=j: invert_sum(j), None)))
                     post.append((lambda x, j=j: has_room(j), True, (None, lambda j=j: e_quantise(j, 0, NCH), None)))
 
         sums = [(j, 0, NCH) for j in range(BT - 1)] + [(BT - 1, g0, g1) for g1, g0 in LAST_GROUPS.items()]
-        done = {"prep": 0, "post": 0, "codes": 0, "sums": 0, "outputs": 0, "sum_at": 0}
+        done = {"prep": 0, "post": 0, "codes": 0, "sums": 0, "outputs": 0}
+        sum_at = {}
 
         def has_room(j):
             return j < done["outputs"] + CODE_BUFS
 
         def place_sum(x):
+            j = done["outputs"]
+            if j in sum_at and (x >= sum_at[j] + SUM_LAG if j < BT - 2 else done["post"] == len(post)):
+                step(lambda: finish(j))
+                done["outputs"] += 1
+                return
             n = done["sums"]
-            if n and sums[n - 1][2] == NCH and done["outputs"] == sums[n - 1][0]:
-                if x >= done["sum_at"] + SUM_LAG:
-                    step(lambda j=done["outputs"]: finish(j))
-                    done["outputs"] += 1
-            elif n < done["codes"] and done["prep"] == len(prep):
+            if n == BT - 2 and done["post"] < len(post) - HOLD:
+                return
+            if n < done["codes"] and done["prep"] == len(prep) and (j not in sum_at or sums[n][0] >= OWN_FROM):
                 step(lambda a=sums[n]: weighted_sum(*a))
                 done["sums"] += 1
-                done["sum_at"] = x
+                if sums[n][2] == NCH:
+                    sum_at[sums[n][0]] = x
 
         def place_piece(x):
             n = done["post"]
@@ -587,17 +590,18 @@ def tile_kanadjunction_pa_kernel(tc, source, target, k_right, WF_right, out):
                 lambda c=c: k_transposes(c),
             )
             if c == 0:
-                step(lambda: (t_out(0), square_t(0), square_t(1)), lambda: t_transposes(0))
-            if c == 1:
-                step(lambda: scale_tt(nc.vector, 0, 2))
+                step(lambda: t_out(0), lambda: t_transposes(0))
 
         for c in range(3):
             key_step(c)
-        step(lambda: [norms_t(a, a + 2) for a in range(2, BT, 2)])
         for c in range(NCH):
             step(lambda c=c: whole_bank(c))
+            if c == SQ_AT:
+                step(lambda: (square_t(0), square_t(1)))
             if c + 3 < NCH:
                 key_step(c + 3)
+            if c == SQ_AT:
+                step(lambda: scale_tt(nc.vector, 0, 2))
             if c >= 1:
                 step(lambda c=c: (clamp_min(c - 1), mark(("bank", c - 1))))
         step(
@@ -617,6 +621,9 @@ def tile_kanadjunction_pa_kernel(tc, source, target, k_right, WF_right, out):
         for x in range(NCH, BT * NCH):
             i, c = x // NCH, x % NCH
             step(lambda x=x: (clamp_min(x), mark(("bank", x)), scores(x + S_BANKS - 1)))
+            if x in NORMS_AT:
+                a = 2 + 2 * NORMS_AT.index(x)
+                step(lambda a=a: norms_t(a, a + 2))
             if c == 0 and i in phase_end:
                 close_phase(phase_end[i], i)
             place_sum(x)

@@ -78,18 +78,21 @@ def tile_kanadjunction_pa_kernel(tc, source, target, k_right, WF_right, out):
         wcodes = keep.tile([P, D], U32, name="wcodes", align_bytes=64)
         wscales = keep.tile([P, D], U8, name="wscales", align_bytes=64)
 
-        k_view = k_right.rearrange("(m p) j -> p m j", p=P)
-        t_view = target.rearrange("(i p) j -> p i j", p=P)
-        s_view = source.rearrange("(a p e) c -> p a (e c)", p=P, e=2)
+        k_view = k_right.rearrange("(q p u) j -> p q u j", p=P, u=2)
+        t_view = target.rearrange("(p i) j -> p i j", p=P)
+        s_view = source.rearrange("(g p e u) c -> p g u e c", p=P, e=2, u=2)
+        out_view = out.rearrange("(p i) d -> p i d", p=P)
         k_nat = [
-            work.tile([P, NT // 2, E], BF16, tag="e", bufs=E_BUFS, name="k_nat%d" % h)
+            work.tile([P, NT // 4, 2, E], BF16, tag="e", bufs=E_BUFS, name="k_nat%d" % h)
             for h in range(2)
         ]
         t_nat = work.tile([P, BT, E], BF16, tag="e", bufs=E_BUFS, name="t_nat")
 
         def load_k(a, b):
-            lo = a % (NT // 2)
-            nc.sync.dma_start(out=k_nat[a // (NT // 2)][:, lo : lo + b - a, :], in_=k_view[:, a:b, :])
+            lo, width = a // 2 % (NT // 4), (b - a) // 2
+            nc.sync.dma_start(
+                out=k_nat[a // (NT // 2)][:, lo : lo + width, :, :], in_=k_view[:, a // 2 : a // 2 + width, :, :]
+            )
 
         load_k(0, 4)
         nc.sync.dma_start(out=t_nat[:, 0:4, :], in_=t_view[:, 0:4, :])
@@ -104,13 +107,14 @@ def tile_kanadjunction_pa_kernel(tc, source, target, k_right, WF_right, out):
 
         def load_src(g):
             src[g] = work.tile([P, 2, C], BF16, tag="src", bufs=SRC_BUFS, name="src")
-            nc.sync.dma_start(out=src[g][:].rearrange("p e c -> p (e c)"), in_=s_view[:, g, :])
+            nc.sync.dma_start(out=src[g][:], in_=s_view[:, g // 2, g % 2, :, :])
 
         for g in range(SRC_BUFS - 1):
             load_src(g)
 
         def k_tile(m):
-            return k_nat[m // 16][:, m % 16, :]
+            c, u, a = m // 4, m // 2 % 2, m % 2
+            return k_nat[c // 4][:, c % 4 * 2 + a, u, :]
 
         def square_rows(rows, total, row):
             nc.scalar.activation(out=junk[:, row % 4, :], in_=rows, func=ACTF.Square, accum_out=total)
@@ -337,11 +341,11 @@ def tile_kanadjunction_pa_kernel(tc, source, target, k_right, WF_right, out):
             nc.vector.reciprocal(rinv[:, j : j + 1], rsum[:, j : j + 1])
 
         def finish(j):
-            o_sb = work.tile([P, D], F32, tag="o_sb", bufs=2, name="o_sb")
+            o_sb = work.tile([P, D], F32, tag="o_sb", bufs=3, name="o_sb")
             nc.vector.tensor_scalar(
                 out=o_sb[:], in0=bank["o", j][:], scalar1=rinv[:, j : j + 1], scalar2=None, op0=ALU.mult
             )
-            nc.sync.dma_start(out=out[P * j : P * j + P, :], in_=o_sb[:])
+            nc.sync.dma_start(out=out_view[:, j, :], in_=o_sb[:])
 
         sgrp = {}
         scodes = {}

@@ -39,6 +39,8 @@ OWN_FROM = BT - 1
 HOLD = 6
 SQ_AT = 0
 NORMS_AT = tuple(range(8, 36, 4))
+WARM_FIRST = 5
+WARM_KEYS = 2
 LATE = tuple((BT - 1, q) for q in range(4))
 
 
@@ -116,6 +118,14 @@ def tile_kanadjunction_pa_kernel(tc, source, target, k_right, WF_right, out):
             c, u, a = m // 4, m // 2 % 2, m % 2
             return k_nat[c // 4][:, c % 4 * 2 + a, u, :]
 
+        zeros = work.tile([P, 512], BF16, tag="egrp", bufs=2, name="zeros", align_bytes=64)
+        nc.vector.memset(zeros[:], 0.0)
+
+        def warm_up(count):
+            for n in range(count):
+                idle = psum.tile([P, 512], F32, tag="s", bufs=S_BANKS, name="idle")
+                nc.tensor.matmul(idle[:], lhsT=zeros[:, 0:P], rhs=zeros[:], start=True, stop=True)
+
         def square_rows(rows, total, row):
             nc.scalar.activation(out=junk[:, row % 4, :], in_=rows, func=ACTF.Square, accum_out=total)
 
@@ -163,6 +173,8 @@ def tile_kanadjunction_pa_kernel(tc, source, target, k_right, WF_right, out):
                     nc.tensor.transpose(
                         pk[:, h, s, :], k_tile(4 * c + s)[:, P * h : P * h + P], ident_b[:]
                     )
+            if c < 3:
+                warm_up(WARM_KEYS)
 
         def k_out(c):
             nc.vector.tensor_copy(
@@ -654,6 +666,7 @@ def tile_kanadjunction_pa_kernel(tc, source, target, k_right, WF_right, out):
                 state["next"] += 1
                 state["open"] += 1
 
+        warm_up(WARM_FIRST)
         feed(-1)
         for now in range(len(steps)):
             ahead, body, ready = steps[now]

@@ -27,7 +27,7 @@ SRC_BUFS = 2
 X_BANKS = 3
 PHASES = (1, 3, 4, 4, 4)
 LEAD = 8
-SPLIT_ROOTS = 3
+SPLIT_ROOTS = 16
 R0 = 0.75
 R1 = 1
 X1 = 48
@@ -41,6 +41,7 @@ SQ_AT = 0
 NORMS_AT = tuple(range(8, 36, 4))
 WARM_FIRST = 5
 WARM_KEYS = 2
+WARM_TAIL = 1
 LATE = tuple((BT - 1, q) for q in range(4))
 
 
@@ -118,7 +119,7 @@ def tile_kanadjunction_pa_kernel(tc, source, target, k_right, WF_right, out):
             c, u, a = m // 4, m // 2 % 2, m % 2
             return k_nat[c // 4][:, c % 4 * 2 + a, u, :]
 
-        zeros = work.tile([P, 512], BF16, tag="egrp", bufs=2, name="zeros", align_bytes=64)
+        zeros = keep.tile([P, 512], BF16, name="zeros")
         nc.vector.memset(zeros[:], 0.0)
 
         def warm_up(count):
@@ -232,13 +233,21 @@ def tile_kanadjunction_pa_kernel(tc, source, target, k_right, WF_right, out):
             for h in range(2):
                 product(x, h)
 
+        mx_queue = []
+
+        def flush_mx():
+            for run in mx_queue:
+                run()
+            mx_queue.clear()
+
         def scores(x):
-            for h in range(2):
-                if x + 1 < BT * NCH:
-                    fold(x + 1, 2 * h)
-                    fold(x + 1, 2 * h + 1)
-                if x < BT * NCH:
-                    product(x, h)
+            if x + 1 < BT * NCH:
+                for s in range(4):
+                    fold(x + 1, s)
+            if x < BT * NCH:
+                product(x, 0)
+                flush_mx()
+                product(x, 1)
 
         def clamp_min(x):
             i, c = x // NCH, x % NCH
@@ -306,6 +315,8 @@ def tile_kanadjunction_pa_kernel(tc, source, target, k_right, WF_right, out):
                 for u in range(2):
                     w0 = 256 * (2 * q + gg) + P * u
                     nc.tensor.transpose(xt[:, gg, u, :], words[:, w0 : w0 + P], ident_f[:])
+            if ("bank", BT * NCH - 1) in seen and q in (0, 2):
+                warm_up(WARM_TAIL)
 
         def e_out(j, q):
             if q == 0:
@@ -413,9 +424,11 @@ def tile_kanadjunction_pa_kernel(tc, source, target, k_right, WF_right, out):
                 in_=sgrp[g][:].rearrange("p t n k -> p (t n k)"),
             )
 
+        def open_f(g, dh):
+            bank["f", g, dh] = psum.tile([P, 4, P], F32, tag="x", bufs=X_BANKS, name="fb")
+
         def f_matmuls(g, dh):
-            fb = psum.tile([P, 4, P], F32, tag="x", bufs=X_BANKS, name="fb")
-            bank["f", g, dh] = fb
+            fb = bank["f", g, dh]
             for t in range(4):
                 nc.tensor.matmul_mx(
                     out=fb[:, t, :],
@@ -510,8 +523,8 @@ def tile_kanadjunction_pa_kernel(tc, source, target, k_right, WF_right, out):
                 prep_item(lambda g=g: s_quantise(g + 1))
             for dh in range(2):
                 prep_item(
-                    lambda g=g, dh=dh: f_out(g, dh),
-                    lambda g=g, dh=dh: f_matmuls(g, dh),
+                    lambda g=g, dh=dh: (flush_mx(), f_out(g, dh)),
+                    lambda g=g, dh=dh: (open_f(g, dh), mx_queue.append(lambda: f_matmuls(g, dh))),
                     lambda g=g: g in scodes,
                 )
         prep_item(lambda: f_quantise(NCH - 1))
@@ -572,14 +585,15 @@ def tile_kanadjunction_pa_kernel(tc, source, target, k_right, WF_right, out):
         def place_sum(x):
             j = done["outputs"]
             if j in sum_at and (x >= sum_at[j] + SUM_LAG if j < BT - 2 else done["post"] == len(post)):
-                step(lambda: finish(j))
+                step(lambda: (flush_mx(), finish(j)))
                 done["outputs"] += 1
                 return
             n = done["sums"]
             if n == BT - 2 and done["post"] < len(post) - HOLD:
                 return
             if n < done["codes"] and done["prep"] == len(prep) and (j not in sum_at or sums[n][0] >= OWN_FROM):
-                step(lambda a=sums[n]: weighted_sum(*a))
+                late = x + S_BANKS > BT * NCH
+                step(lambda a=sums[n], late=late: (mx_queue.append(lambda: weighted_sum(*a)), flush_mx() if late else None))
                 done["sums"] += 1
                 if sums[n][2] == NCH:
                     sum_at[sums[n][0]] = x

@@ -62,7 +62,7 @@ def tile_kanadjunction_pa_kernel(tc, source, target, k_right, WF_right, out):
         warm = keep.tile([P, 1], F32, name="warm")
         nc.scalar.activation(out=warm[:], in_=one[:], func=ACTF.Sqrt)
 
-        kT = keep.tile([P, 2, N], BF16, name="kT")
+        kT = keep.tile([P, N], F32, name="kT")
         tT = keep.tile([P, 2, B], BF16, name="tT")
         kk = keep.tile([P, NT], F32, name="kk")
         tt = keep.tile([P, TT_PAD + BT], F32, name="tt")
@@ -167,20 +167,17 @@ def tile_kanadjunction_pa_kernel(tc, source, target, k_right, WF_right, out):
         bank = {}
 
         def k_transposes(c):
-            pk = psum.tile([P, 2, 4, P], BF16, tag="x", bufs=X_BANKS, name="pk")
+            pk = psum.tile([P, 4, P], F32, tag="x", bufs=X_BANKS, name="pk")
             bank["k", c] = pk
             for s in range(4):
-                for h in range(2):
-                    nc.tensor.transpose(
-                        pk[:, h, s, :], k_tile(4 * c + s)[:, P * h : P * h + P], ident_b[:]
-                    )
+                nc.tensor.transpose(pk[:, s, :], k_tile(4 * c + s).bitcast(F32), ident_f[:])
             if c < 3:
                 warm_up(WARM_KEYS)
 
         def k_out(c):
             nc.vector.tensor_copy(
-                out=kT[:, :, 512 * c : 512 * c + 512],
-                in_=bank["k", c][:].rearrange("p h s n -> p h (s n)"),
+                out=kT[:, 512 * c : 512 * c + 512],
+                in_=bank["k", c][:].rearrange("p s n -> p (s n)"),
             )
 
         def t_transposes(a):
@@ -188,9 +185,7 @@ def tile_kanadjunction_pa_kernel(tc, source, target, k_right, WF_right, out):
             bank["t", a] = pt
             for s in range(4):
                 for h in range(2):
-                    nc.tensor.transpose(
-                        pt[:, h, s, :], t_nat[:, 4 * a + s, P * h : P * h + P], ident_b[:]
-                    )
+                    nc.tensor.transpose(pt[:, h, s, :], t_nat[:, 4 * a + s, h : E : 2], ident_b[:])
 
         def t_out(a):
             nc.vector.tensor_scalar(
@@ -222,7 +217,7 @@ def tile_kanadjunction_pa_kernel(tc, source, target, k_right, WF_right, out):
             nc.tensor.matmul(
                 bank["s", x][:],
                 lhsT=tT[:, h, P * i : P * i + P],
-                rhs=kT[:, h, 512 * c : 512 * c + 512],
+                rhs=kT[:, 512 * c : 512 * c + 512].bitcast(BF16).rearrange("p (n h) -> p h n", h=2)[:, h, :],
                 start=False,
                 stop=(h == 1),
             )

@@ -24,7 +24,7 @@ ZR_BUFS = 6
 E_BUFS = 6
 S_BANKS = 4
 SRC_BUFS = 2
-X_BANKS = 3
+X_BANKS = 4
 PHASES = (1, 3, 4, 4, 4)
 LEAD = 8
 SPLIT_ROOTS = 16
@@ -32,10 +32,10 @@ R0 = 0.75
 R1 = 1
 X1 = 48
 POST_LAG = 24
-POST_CAP = 1.5
+POST_CAP = 2
 SUM_LAG = 4
 CODE_BUFS = 3
-OWN_FROM = BT - 1
+OWN_FROM = BT - 2
 HOLD = 6
 SQ_AT = 0
 NORMS_AT = tuple(range(8, 36, 4))
@@ -333,13 +333,11 @@ def tile_kanadjunction_pa_kernel(tc, source, target, k_right, WF_right, out):
                 scales=escales[j][:, P * g0 : P * g1],
                 in_=egrp[j][:, g0:g1, :, :].rearrange("p g b t -> p (g b t)"),
             )
+            mark(("codes", j))
 
         def weighted_sum(j, g0, g1):
-            if g0 == 0:
-                if j < OWN_FROM:
-                    bank["o", j] = psum.tile([P, D], F32, tag="o", bufs=1, name="po")
-                else:
-                    bank["o", j] = psum.tile([P, D], F32, tag="s", bufs=S_BANKS, name="po_last")
+            if g0 == 0 and j >= OWN_FROM:
+                bank["o", j] = psum.tile([P, D], F32, tag="s", bufs=S_BANKS, name="po_last")
             po = bank["o", j]
             for g in range(g0, g1):
                 nc.tensor.matmul_mx(
@@ -351,6 +349,12 @@ def tile_kanadjunction_pa_kernel(tc, source, target, k_right, WF_right, out):
                     start=(g == 0),
                     stop=(g == NCH - 1),
                 )
+
+        def open_sum(j):
+            bank["o", j] = psum.tile([P, D], F32, tag="x", bufs=X_BANKS, name="po")
+            mx_queue.append(lambda: weighted_sum(j, 0, NCH))
+            if ("scores", BT * NCH) in seen:
+                flush_mx()
 
         def add_last_sums():
             nc.vector.tensor_reduce(out=rsum[:, BT - 1 : BT], in_=rsum_last[:], axis=AX.X, op=ALU.add)
@@ -522,7 +526,7 @@ def tile_kanadjunction_pa_kernel(tc, source, target, k_right, WF_right, out):
                     lambda g=g, dh=dh: (open_f(g, dh), mx_queue.append(lambda: f_matmuls(g, dh))),
                     lambda g=g: g in scodes,
                 )
-        prep_item(lambda: f_quantise(NCH - 1))
+        prep_item(lambda: (f_quantise(NCH - 1), mark("f")))
 
         phase_end = {}
         phase_of = {}
@@ -572,26 +576,32 @@ def tile_kanadjunction_pa_kernel(tc, source, target, k_right, WF_right, out):
 
         sums = [(j, 0, NCH) for j in range(BT - 1)] + [(BT - 1, g0, g1) for g1, g0 in LAST_GROUPS.items()]
         done = {"prep": 0, "post": 0, "codes": 0, "sums": 0, "outputs": 0}
-        sum_at = {}
+        codes_at = {}
 
         def has_room(j):
             return j < done["outputs"] + CODE_BUFS
 
         def place_sum(x):
             j = done["outputs"]
-            if j in sum_at and (x >= sum_at[j] + SUM_LAG if j < BT - 2 else done["post"] == len(post)):
-                step(lambda: (flush_mx(), finish(j)))
-                done["outputs"] += 1
+            if j < OWN_FROM:
+                if done["codes"] > j and done["prep"] == len(prep):
+                    codes_at.setdefault(j, x)
+                    if x >= codes_at[j] + SUM_LAG:
+                        step(
+                            lambda: (flush_mx(), finish(j)),
+                            lambda: open_sum(j),
+                            lambda: ("codes", j) in seen and "f" in seen,
+                        )
+                        done["outputs"] += 1
+                        done["sums"] += 1
                 return
             n = done["sums"]
-            if n == BT - 2 and done["post"] < len(post) - HOLD:
-                return
-            if n < done["codes"] and done["prep"] == len(prep) and (j not in sum_at or sums[n][0] >= OWN_FROM):
-                late = x + S_BANKS > BT * NCH
-                step(lambda a=sums[n], late=late: (mx_queue.append(lambda: weighted_sum(*a)), flush_mx() if late else None))
+            if n < len(sums) and n < done["codes"] and not (n == BT - 2 and done["post"] < len(post) - HOLD):
+                step(lambda a=sums[n]: weighted_sum(*a))
                 done["sums"] += 1
-                if sums[n][2] == NCH:
-                    sum_at[sums[n][0]] = x
+            elif n == len(sums) and done["post"] == len(post):
+                step(lambda: finish(j))
+                done["outputs"] += 1
 
         def place_piece(x):
             n = done["post"]
@@ -645,7 +655,7 @@ def tile_kanadjunction_pa_kernel(tc, source, target, k_right, WF_right, out):
         credit = 0
         for x in range(NCH, BT * NCH):
             i, c = x // NCH, x % NCH
-            step(lambda x=x: (clamp_min(x), mark(("bank", x)), scores(x + S_BANKS - 1)))
+            step(lambda x=x: (clamp_min(x), mark(("bank", x)), scores(x + S_BANKS - 1), mark(("scores", x + S_BANKS - 1))))
             if x in NORMS_AT:
                 a = 2 + 2 * NORMS_AT.index(x)
                 step(lambda a=a: norms_t(a, a + 2))

@@ -30,7 +30,7 @@ LEAD = 8
 SPLIT_ROOTS = 16
 R0 = 0.75
 R1 = 1
-X1 = 48
+X1 = 56
 POST_LAG = 24
 POST_CAP = 2
 SUM_LAG = 4
@@ -38,10 +38,12 @@ CODE_BUFS = 3
 OWN_FROM = BT - 2
 HOLD = 6
 SQ_AT = 0
-NORMS_AT = tuple(range(8, 36, 4))
+T_GROUPS = ((2, 6), (6, 11), (11, 16))
 WARM_FIRST = 5
 WARM_KEYS = 2
 WARM_TAIL = 1
+S_SCALAR = ((2, 0),)
+F_SCALAR = ((0, 0),)
 LATE = tuple((BT - 1, q) for q in range(4))
 
 
@@ -160,8 +162,21 @@ def tile_kanadjunction_pa_kernel(tc, source, target, k_right, WF_right, out):
                 )
 
         def norms_t(a, b):
-            for i in range(a, b):
-                square_rows(t_nat[:, i, :], columns(tt, i, i + 1), i)
+            part = t_nat[:, a:b, :]
+            sq = work.tile([P, 7, E], F32, tag="egrp", bufs=2, name="sq_t", align_bytes=64)
+            nc.gpsimd.tensor_tensor(out=sq[:, 0 : b - a, :], in0=part, in1=part, op=ALU.mult)
+            width = E // 2
+            while width > 1:
+                nc.gpsimd.tensor_tensor(
+                    out=sq[:, 0 : b - a, 0:width],
+                    in0=sq[:, 0 : b - a, 0:width],
+                    in1=sq[:, 0 : b - a, width : 2 * width],
+                    op=ALU.add,
+                )
+                width //= 2
+            nc.gpsimd.tensor_tensor(
+                out=columns(tt, a, b), in0=sq[:, 0 : b - a, 0], in1=sq[:, 0 : b - a, 1], op=ALU.add
+            )
             scale_tt(nc.gpsimd, a, b)
 
         bank = {}
@@ -407,7 +422,8 @@ def tile_kanadjunction_pa_kernel(tc, source, target, k_right, WF_right, out):
         def s_out(g, half):
             if half == 0:
                 sgrp[g] = work.tile([P, 4, P, 4], BF16, tag="sgrp", bufs=1, name="sgrp", align_bytes=64)
-            nc.vector.tensor_copy(
+            copy = nc.scalar.copy if (g, half) in S_SCALAR else nc.vector.tensor_copy
+            copy(
                 out=sgrp[g][:].bitcast(F32)[:, 2 * half : 2 * half + 2, :, :],
                 in_=bank["src", g, half][:].rearrange("p t u n -> p t n u"),
             )
@@ -442,7 +458,8 @@ def tile_kanadjunction_pa_kernel(tc, source, target, k_right, WF_right, out):
         def f_out(g, dh):
             if dh == 0:
                 fgrp[g] = work.tile([P, D, 4], BF16, tag="fgrp", bufs=1, name="fgrp", align_bytes=64)
-            nc.vector.tensor_copy(
+            copy = nc.scalar.copy if (g, dh) in F_SCALAR else nc.vector.tensor_copy
+            copy(
                 out=fgrp[g][:, P * dh : P * dh + P, :],
                 in_=bank["f", g, dh][:].rearrange("p t d -> p d t"),
             )
@@ -627,6 +644,8 @@ def tile_kanadjunction_pa_kernel(tc, source, target, k_right, WF_right, out):
             if c == 0:
                 step(lambda: t_out(0), lambda: t_transposes(0))
 
+        for a, b in T_GROUPS:
+            step(lambda a=a, b=b: norms_t(a, b))
         for c in range(3):
             key_step(c)
         for c in range(NCH):
@@ -656,9 +675,6 @@ def tile_kanadjunction_pa_kernel(tc, source, target, k_right, WF_right, out):
         for x in range(NCH, BT * NCH):
             i, c = x // NCH, x % NCH
             step(lambda x=x: (clamp_min(x), mark(("bank", x)), scores(x + S_BANKS - 1), mark(("scores", x + S_BANKS - 1))))
-            if x in NORMS_AT:
-                a = 2 + 2 * NORMS_AT.index(x)
-                step(lambda a=a: norms_t(a, a + 2))
             if c == 0 and i in phase_end:
                 close_phase(phase_end[i], i)
             place_sum(x)

@@ -38,7 +38,8 @@ CODE_BUFS = 3
 OWN_FROM = BT - 2
 HOLD = 6
 SQ_AT = 0
-T_GROUPS = ((2, 6), (6, 11), (11, 16))
+T_GROUPS = ((2, 9),)
+NORMS_AT = {28: (9, 16)}
 WARM_FIRST = 5
 WARM_KEYS = 2
 WARM_TAIL = 1
@@ -177,6 +178,11 @@ def tile_kanadjunction_pa_kernel(tc, source, target, k_right, WF_right, out):
             nc.gpsimd.tensor_tensor(
                 out=columns(tt, a, b), in0=sq[:, 0 : b - a, 0], in1=sq[:, 0 : b - a, 1], op=ALU.add
             )
+            scale_tt(nc.gpsimd, a, b)
+
+        def scalar_norms(a, b):
+            for i in range(a, b):
+                square_rows(t_nat[:, i, :], columns(tt, i, i + 1), i)
             scale_tt(nc.gpsimd, a, b)
 
         bank = {}
@@ -675,6 +681,8 @@ def tile_kanadjunction_pa_kernel(tc, source, target, k_right, WF_right, out):
         for x in range(NCH, BT * NCH):
             i, c = x // NCH, x % NCH
             step(lambda x=x: (clamp_min(x), mark(("bank", x)), scores(x + S_BANKS - 1), mark(("scores", x + S_BANKS - 1))))
+            if x in NORMS_AT:
+                step(lambda ab=NORMS_AT[x]: scalar_norms(*ab))
             if c == 0 and i in phase_end:
                 close_phase(phase_end[i], i)
             place_sum(x)

from contextlib import ExitStack

import concourse.mybir as mybir
from concourse.masks import make_identity

F32 = mybir.dt.float32
BF16 = mybir.dt.bfloat16
U32 = mybir.dt.uint32
U8 = mybir.dt.uint8
FP8X4 = mybir.dt.float8_e4m3fn_x4
ALU = mybir.AluOpType
ACTF = mybir.ActivationFunctionType
AX = mybir.AxisListType

P = 128
N, B, C, E, D = 4096, 2048, 512, 256, 256
NT = N // P
BT = B // P
TT_PAD = 6
NCH = N // 512
FLOPS = 2 * (N * C * D + 2 * B * N * E)

ZR_BUFS = 6
E_BUFS = 6
S_BANKS = 4
SRC_BUFS = 2
X_BANKS = 4
PHASES = (1, 3, 4, 4, 4)
LEAD = 8
SPLIT_ROOTS = 16
R0 = 0.75
R1 = 1
X1 = 56
POST_LAG = 24
POST_CAP = 2
SUM_LAG = 4
CODE_BUFS = 3
OWN_FROM = BT - 2
HOLD = 6
SQ_AT = 0
T_GROUPS = ((2, 9),)
NORMS_AT = {28: (9, 16)}
WARM_FIRST = 5
WARM_KEYS = 2
WARM_TAIL = 1
S_SCALAR = ((2, 0),)
F_SCALAR = ((0, 0),)
LATE = tuple((BT - 1, q) for q in range(4))


def tile_kanadjunction_pa_kernel(tc, source, target, k_right, WF_right, out):
    nc = tc.nc
    with ExitStack() as ctx:
        keep = ctx.enter_context(tc.tile_pool(name="keep", bufs=1))
        work = ctx.enter_context(tc.tile_pool(name="work", bufs=1))
        psum = ctx.enter_context(tc.psum_pool(name="psum", bufs=1))
        ctx.enter_context(tc.manual_schedule())

        ident_b = keep.tile([P, P], BF16, name="ident_b")
        make_identity(nc, ident_b[:])
        ident_f = keep.tile([P, P], F32, name="ident_f")
        make_identity(nc, ident_f[:])
        one = keep.tile([P, 1], F32, name="one")
        nc.vector.memset(one[:], 1.0)
        warm = keep.tile([P, 1], F32, name="warm")
        nc.scalar.activation(out=warm[:], in_=one[:], func=ACTF.Sqrt)

        kT = keep.tile([P, N], F32, name="kT")
        tT = keep.tile([P, 2, B], BF16, name="tT")
        kk = keep.tile([P, NT], F32, name="kk")
        tt = keep.tile([P, TT_PAD + BT], F32, name="tt")
        negtt = keep.tile([P, TT_PAD + BT], F32, name="negtt")
        tt256 = keep.tile([P, TT_PAD + BT], F32, name="tt256")
        zm8 = keep.tile([P, BT, NCH], F32, name="zm8")
        zmin = keep.tile([P, BT], F32, name="zmin")
        bexp = keep.tile([P, BT], F32, name="bexp")
        rsum_last = keep.tile([P, 3], F32, name="rsum_last")
        rsum = keep.tile([P, BT], F32, name="rsum")
        rinv = keep.tile([P, BT], F32, name="rinv")
        junk_v = keep.tile([P, 2, E], F32, name="junk_v")
        junk = keep.tile([P, 4, E], BF16, name="junk")
        fcodes = keep.tile([P, NCH, D], U32, name="fcodes", align_bytes=64)
        fscales = keep.tile([P, NCH, D], U8, name="fscales", align_bytes=64)
        wcodes = keep.tile([P, D], U32, name="wcodes", align_bytes=64)
        wscales = keep.tile([P, D], U8, name="wscales", align_bytes=64)

        k_view = k_right.rearrange("(q p u) j -> p q u j", p=P, u=2)
        t_view = target.rearrange("(p i) j -> p i j", p=P)
        s_view = source.rearrange("(g p e u) c -> p g u e c", p=P, e=2, u=2)
        out_view = out.rearrange("(p i) d -> p i d", p=P)
        k_nat = [
            work.tile([P, NT // 4, 2, E], BF16, tag="e", bufs=E_BUFS, name="k_nat%d" % h)
            for h in range(2)
        ]
        t_nat = work.tile([P, BT, E], BF16, tag="e", bufs=E_BUFS, name="t_nat")

        def load_k(a, b):
            lo, width = a // 2 % (NT // 4), (b - a) // 2
            nc.sync.dma_start(
                out=k_nat[a // (NT // 2)][:, lo : lo + width, :, :], in_=k_view[:, a // 2 : a // 2 + width, :, :]
            )

        load_k(0, 4)
        nc.sync.dma_start(out=t_nat[:, 0:4, :], in_=t_view[:, 0:4, :])
        for a, b in ((4, 8), (8, 16), (16, 24), (24, 32)):
            load_k(a, b)
        nc.sync.dma_start(out=t_nat[:, 4:BT, :], in_=t_view[:, 4:BT, :])
        wf_nat = work.tile([P, 2, C], BF16, tag="src", bufs=SRC_BUFS, name="wf_nat")
        nc.sync.dma_start(out=wf_nat[:], in_=WF_right.rearrange("(h p) c -> p h c", p=P))
        wgrp = work.tile([P, D, 4], BF16, tag="fgrp", bufs=1, name="wgrp", align_bytes=64)

        src = {}

        def load_src(g):
            src[g] = work.tile([P, 2, C], BF16, tag="src", bufs=SRC_BUFS, name="src")
            nc.sync.dma_start(out=src[g][:], in_=s_view[:, g // 2, g % 2, :, :])

        for g in range(SRC_BUFS - 1):
            load_src(g)

        def k_tile(m):
            c, u, a = m // 4, m // 2 % 2, m % 2
            return k_nat[c // 4][:, c % 4 * 2 + a, u, :]

        zeros = keep.tile([P, 512], BF16, name="zeros")
        nc.vector.memset(zeros[:], 0.0)

        def warm_up(count):
            for n in range(count):
                idle = psum.tile([P, 512], F32, tag="s", bufs=S_BANKS, name="idle")
                nc.tensor.matmul(idle[:], lhsT=zeros[:, 0:P], rhs=zeros[:], start=True, stop=True)

        def square_rows(rows, total, row):
            nc.scalar.activation(out=junk[:, row % 4, :], in_=rows, func=ACTF.Square, accum_out=total)

        def square_k(m):
            square_rows(k_tile(m), kk[:, m : m + 1], m)

        def columns(norms, a, b):
            pad = 0 if b <= 2 else TT_PAD
            return norms[:, pad + a : pad + b]

        def square_t(i):
            nc.vector.scalar_tensor_tensor(
                out=junk_v[:, i, :],
                in0=t_nat[:, i, :],
                scalar=1.0,
                in1=t_nat[:, i, :],
                op0=ALU.mult,
                op1=ALU.mult,
                accum_out=columns(tt, i, i + 1),
            )

        def scale_tt(engine, a, b):
            for out, factor in ((negtt, -1.0), (tt256, 1.0 / 256.0)):
                engine.tensor_scalar(
                    out=columns(out, a, b),
                    in0=columns(tt, a, b),
                    scalar1=factor,
                    scalar2=0.0,
                    op0=ALU.mult,
                    op1=ALU.add,
                )

        def norms_t(a, b):
            part = t_nat[:, a:b, :]
            sq = work.tile([P, 7, E], F32, tag="egrp", bufs=2, name="sq_t", align_bytes=64)
            nc.gpsimd.tensor_tensor(out=sq[:, 0 : b - a, :], in0=part, in1=part, op=ALU.mult)
            width = E // 2
            while width > 1:
                nc.gpsimd.tensor_tensor(
                    out=sq[:, 0 : b - a, 0:width],
                    in0=sq[:, 0 : b - a, 0:width],
                    in1=sq[:, 0 : b - a, width : 2 * width],
                    op=ALU.add,
                )
                width //= 2
            nc.gpsimd.tensor_tensor(
                out=columns(tt, a, b), in0=sq[:, 0 : b - a, 0], in1=sq[:, 0 : b - a, 1], op=ALU.add
            )
            scale_tt(nc.gpsimd, a, b)

        def scalar_norms(a, b):
            for i in range(a, b):
                square_rows(t_nat[:, i, :], columns(tt, i, i + 1), i)
            scale_tt(nc.gpsimd, a, b)

        bank = {}

        def k_transposes(c):
            pk = psum.tile([P, 4, P], F32, tag="x", bufs=X_BANKS, name="pk")
            bank["k", c] = pk
            for s in range(4):
                nc.tensor.transpose(pk[:, s, :], k_tile(4 * c + s).bitcast(F32), ident_f[:])
            if c < 3:
                warm_up(WARM_KEYS)

        def k_out(c):
            nc.vector.tensor_copy(
                out=kT[:, 512 * c : 512 * c + 512],
                in_=bank["k", c][:].rearrange("p s n -> p (s n)"),
            )

        def t_transposes(a):
            pt = psum.tile([P, 2, 4, P], BF16, tag="x", bufs=X_BANKS, name="pt")
            bank["t", a] = pt
            for s in range(4):
                for h in range(2):
                    nc.tensor.transpose(pt[:, h, s, :], t_nat[:, 4 * a + s, h : E : 2], ident_b[:])

        def t_out(a):
            nc.vector.tensor_scalar(
                out=tT[:, :, 512 * a : 512 * a + 512],
                in0=bank["t", a][:].rearrange("p h s n -> p h (s n)"),
                scalar1=-2.0,
                scalar2=None,
                op0=ALU.mult,
            )

        zr = {}

        def fold(x, s):
            c = x % NCH
            if s == 0:
                bank["s", x] = psum.tile([P, 512], F32, tag="s", bufs=S_BANKS, name="sp")
            m = 4 * c + s
            nc.tensor.matmul(
                bank["s", x][:, P * s : P * s + P],
                lhsT=kk[:, m : m + 1].to_broadcast([P, P]),
                rhs=ident_f[:],
                is_transpose=True,
                start=(s == 0),
                stop=False,
            )

        def product(x, h):
            i, c = x // NCH, x % NCH
            nc.tensor.matmul(
                bank["s", x][:],
                lhsT=tT[:, h, P * i : P * i + P],
                rhs=kT[:, 512 * c : 512 * c + 512].bitcast(BF16).rearrange("p (n h) -> p h n", h=2)[:, h, :],
                start=False,
                stop=(h == 1),
            )

        def whole_bank(x):
            for s in range(4):
                fold(x, s)
            for h in range(2):
                product(x, h)

        mx_queue = []

        def flush_mx():
            for run in mx_queue:
                run()
            mx_queue.clear()

        def scores(x):
            if x + 1 < BT * NCH:
                for s in range(4):
                    fold(x + 1, s)
            if x < BT * NCH:
                product(x, 0)
                flush_mx()
                product(x, 1)

        def clamp_min(x):
            i, c = x // NCH, x % NCH
            if c == 0:
                zr[i] = work.tile([P, N], F32, tag="zr", bufs=ZR_BUFS, name="zr")
            nc.vector.tensor_scalar(
                out=zr[i][:, 512 * c : 512 * c + 512],
                in0=bank["s", x][:],
                scalar1=columns(negtt, i, i + 1),
                scalar2=None,
                op0=ALU.max,
                op1=ALU.min,
                accum_out=zm8[:, i, c : c + 1],
            )

        def row_min(a, b):
            nc.vector.tensor_reduce(out=zmin[:, a:b], in_=zm8[:, a:b, :], axis=AX.X, op=ALU.min)

        def root(i, lo, hi):
            nc.scalar.activation(
                out=zr[i][:, lo:hi], in_=zr[i][:, lo:hi], func=ACTF.Sqrt, bias=columns(tt, i, i + 1), scale=1.0
            )

        def shifts(a, b):
            for i in range(a, b):
                nc.scalar.activation(
                    out=bexp[:, i : i + 1],
                    in_=zmin[:, i : i + 1],
                    func=ACTF.Sqrt,
                    bias=columns(tt256, i, i + 1),
                    scale=1.0 / 256.0,
                )

        e_sb = {}

        def expo(i):
            e_sb[i] = work.tile([P, N], BF16, tag="e", bufs=E_BUFS, name="e_sb")
            if i < BT - 1:
                pieces = [(0, N, rsum[:, i : i + 1])]
            else:
                pieces = [
                    (0, N // 2, rsum_last[:, 0:1]),
                    (N // 2, 3 * N // 4, rsum_last[:, 1:2]),
                    (3 * N // 4, N, rsum_last[:, 2:3]),
                ]
            for lo, hi, total in pieces:
                nc.scalar.activation(
                    out=e_sb[i][:, lo:hi],
                    in_=zr[i][:, lo:hi],
                    func=ACTF.Exp,
                    bias=bexp[:, i : i + 1],
                    scale=-1.0 / 16.0,
                    accum_out=total,
                )

        egrp = {}
        ecodes = {}
        escales = {}

        def e_transposes(j, q):
            xt = psum.tile([P, 2, 2, P], F32, tag="x", bufs=X_BANKS, name="xt")
            bank["e", j, q] = xt
            words = e_sb[j][:].bitcast(F32)
            for gg in range(2):
                for u in range(2):
                    w0 = 256 * (2 * q + gg) + P * u
                    nc.tensor.transpose(xt[:, gg, u, :], words[:, w0 : w0 + P], ident_f[:])
            if ("bank", BT * NCH - 1) in seen and q in (0, 2):
                warm_up(WARM_TAIL)

        def e_out(j, q):
            if q == 0:
                egrp[j] = work.tile(
                    [P, NCH, P, 4], BF16, tag="egrp", bufs=2, name="egrp", align_bytes=64
                )
            copy = nc.scalar.copy if (j, q) in LATE else nc.vector.tensor_copy
            copy(
                out=egrp[j][:].bitcast(F32)[:, 2 * q : 2 * q + 2, :, :],
                in_=bank["e", j, q][:].rearrange("p g u b -> p g b u"),
            )

        def e_quantise(j, g0, g1):
            if g0 == 0:
                ecodes[j] = work.tile([P, NCH * P], U32, tag="ecodes", bufs=CODE_BUFS, name="ecodes", align_bytes=64)
                escales[j] = work.tile([P, NCH * P], U8, tag="escales", bufs=CODE_BUFS, name="escales", align_bytes=64)
            nc.vector.quantize_mx(
                out=ecodes[j][:, P * g0 : P * g1].bitcast(FP8X4),
                scales=escales[j][:, P * g0 : P * g1],
                in_=egrp[j][:, g0:g1, :, :].rearrange("p g b t -> p (g b t)"),
            )
            mark(("codes", j))

        def weighted_sum(j, g0, g1):
            if g0 == 0 and j >= OWN_FROM:
                bank["o", j] = psum.tile([P, D], F32, tag="s", bufs=S_BANKS, name="po_last")
            po = bank["o", j]
            for g in range(g0, g1):
                nc.tensor.matmul_mx(
                    out=po[:],
                    lhsT=ecodes[j][:, P * g : P * g + P].bitcast(FP8X4),
                    lhsT_scale=escales[j][:, P * g : P * g + P],
                    rhs=fcodes[:, g, :].bitcast(FP8X4),
                    rhs_scale=fscales[:, g, :],
                    start=(g == 0),
                    stop=(g == NCH - 1),
                )

        def open_sum(j):
            bank["o", j] = psum.tile([P, D], F32, tag="x", bufs=X_BANKS, name="po")
            mx_queue.append(lambda: weighted_sum(j, 0, NCH))
            if ("scores", BT * NCH) in seen:
                flush_mx()

        def add_last_sums():
            nc.vector.tensor_reduce(out=rsum[:, BT - 1 : BT], in_=rsum_last[:], axis=AX.X, op=ALU.add)

        def invert_sum(j):
            nc.vector.reciprocal(rinv[:, j : j + 1], rsum[:, j : j + 1])

        def finish(j):
            o_sb = work.tile([P, D], F32, tag="o_sb", bufs=3, name="o_sb")
            nc.vector.tensor_scalar(
                out=o_sb[:], in0=bank["o", j][:], scalar1=rinv[:, j : j + 1], scalar2=None, op0=ALU.mult
            )
            nc.sync.dma_start(out=out_view[:, j, :], in_=o_sb[:])

        sgrp = {}
        scodes = {}
        sscales = {}
        fgrp = {}

        def w_transposes():
            xw = psum.tile([P, 2, 2, P], F32, tag="x", bufs=X_BANKS, name="xw")
            bank["w"] = xw
            words = wf_nat[:].bitcast(F32)
            for h in range(2):
                for u in range(2):
                    nc.tensor.transpose(xw[:, h, u, :], words[:, h, P * u : P * u + P], ident_f[:])

        def w_out():
            nc.vector.tensor_copy(
                out=wgrp[:].bitcast(F32).rearrange("p (h d) u -> p h d u", h=2),
                in_=bank["w"][:].rearrange("p h u d -> p h d u"),
            )
            load_src(SRC_BUFS - 1)

        def w_quantise():
            nc.vector.quantize_mx(
                out=wcodes[:].bitcast(FP8X4),
                scales=wscales[:],
                in_=wgrp[:].rearrange("p d t -> p (d t)"),
            )

        def s_transposes(g, half):
            xs = psum.tile([P, 2, 2, P], F32, tag="x", bufs=X_BANKS, name="xs")
            bank["src", g, half] = xs
            words = src[2 * g + half][:].bitcast(F32)
            for tl in range(2):
                for u in range(2):
                    nc.tensor.transpose(xs[:, tl, u, :], words[:, tl, P * u : P * u + P], ident_f[:])

        def s_out(g, half):
            if half == 0:
                sgrp[g] = work.tile([P, 4, P, 4], BF16, tag="sgrp", bufs=1, name="sgrp", align_bytes=64)
            copy = nc.scalar.copy if (g, half) in S_SCALAR else nc.vector.tensor_copy
            copy(
                out=sgrp[g][:].bitcast(F32)[:, 2 * half : 2 * half + 2, :, :],
                in_=bank["src", g, half][:].rearrange("p t u n -> p t n u"),
            )
            if 2 * g + half + SRC_BUFS < 2 * NCH:
                load_src(2 * g + half + SRC_BUFS)

        def s_quantise(g):
            scodes[g] = work.tile([P, 4 * P], U32, tag="scodes", bufs=2, name="scodes", align_bytes=64)
            sscales[g] = work.tile([P, 4 * P], U8, tag="sscales", bufs=2, name="sscales", align_bytes=64)
            nc.vector.quantize_mx(
                out=scodes[g][:].bitcast(FP8X4),
                scales=sscales[g][:],
                in_=sgrp[g][:].rearrange("p t n k -> p (t n k)"),
            )

        def open_f(g, dh):
            bank["f", g, dh] = psum.tile([P, 4, P], F32, tag="x", bufs=X_BANKS, name="fb")

        def f_matmuls(g, dh):
            fb = bank["f", g, dh]
            for t in range(4):
                nc.tensor.matmul_mx(
                    out=fb[:, t, :],
                    lhsT=scodes[g][:, P * t : P * t + P].bitcast(FP8X4),
                    lhsT_scale=sscales[g][:, P * t : P * t + P],
                    rhs=wcodes[:, P * dh : P * dh + P].bitcast(FP8X4),
                    rhs_scale=wscales[:, P * dh : P * dh + P],
                    start=True,
                    stop=True,
                )

        def f_out(g, dh):
            if dh == 0:
                fgrp[g] = work.tile([P, D, 4], BF16, tag="fgrp", bufs=1, name="fgrp", align_bytes=64)
            copy = nc.scalar.copy if (g, dh) in F_SCALAR else nc.vector.tensor_copy
            copy(
                out=fgrp[g][:, P * dh : P * dh + P, :],
                in_=bank["f", g, dh][:].rearrange("p t d -> p d t"),
            )

        def f_quantise(g):
            nc.vector.quantize_mx(
                out=fcodes[:, g, :].bitcast(FP8X4),
                scales=fscales[:, g, :],
                in_=fgrp[g][:].rearrange("p d t -> p (d t)"),
            )

        steps = []
        seen = set()

        act_queue = []
        first = 0
        for size in PHASES:
            for t in range(first, first + size):
                if t < SPLIT_ROOTS:
                    act_queue.append(("root", t, 0, N // 2))
                    act_queue.append(("root", t, N // 2, N))
                else:
                    act_queue.append(("root", t, 0, N))
            act_queue.append(("shifts", first, first + size, 0))
            act_queue.extend([("exp", t, 0, 0) for t in range(first, first + size)])
            first += size
        act_state = {"next": 0}

        def pump_act():
            while act_state["next"] < len(act_queue):
                kind, t, lo, hi = act_queue[act_state["next"]]
                if kind == "root":
                    if ("bank", NCH * t + hi // 512 - 1) not in seen:
                        break
                    root(t, lo, hi)
                elif kind == "shifts":
                    if ("shift", lo) not in seen:
                        break
                    shifts(t, lo)
                else:
                    if t >= E_BUFS and ("turned", t - E_BUFS) not in seen:
                        break
                    expo(t)
                act_state["next"] += 1

        def step(body, ahead=None, ready=None):
            steps.append((ahead, body, ready))

        def mark(key):
            seen.add(key)

        prep = []

        def prep_item(body, ahead=None, ready=None):
            prep.append((ahead, body, ready))

        def source_items(g):
            for half in range(2):
                prep_item(
                    lambda g=g, half=half: s_out(g, half),
                    lambda g=g, half=half: s_transposes(g, half),
                    lambda g=g, half=half: 2 * g + half in src,
                )

        for a in range(1, BT // 4):
            prep_item(lambda a=a: t_out(a), lambda a=a: t_transposes(a))
        prep_item(w_out, w_transposes)
        source_items(0)
        prep_item(w_quantise)
        prep_item(lambda: s_quantise(0))
        for g in range(NCH):
            if g + 1 < NCH:
                source_items(g + 1)
            if g >= 1:
                prep_item(lambda g=g: f_quantise(g - 1))
            if g + 1 < NCH:
                prep_item(lambda g=g: s_quantise(g + 1))
            for dh in range(2):
                prep_item(
                    lambda g=g, dh=dh: (flush_mx(), f_out(g, dh)),
                    lambda g=g, dh=dh: (open_f(g, dh), mx_queue.append(lambda: f_matmuls(g, dh))),
                    lambda g=g: g in scodes,
                )
        prep_item(lambda: (f_quantise(NCH - 1), mark("f")))

        phase_end = {}
        phase_of = {}
        first = 0
        for size in PHASES:
            phase_end[first + size] = first
            for j in range(first, first + size):
                phase_of[j] = (first, first + size)
            first += size

        def earliest(j):
            if j == BT:
                return 2 * BT * NCH
            a, b = phase_of[j]
            return NCH * b + 4 * (j - a) + POST_LAG

        last_phase = phase_end[BT]
        LAST_GROUPS = {4: 0, 6: 4, 8: 6}
        post = []
        for j in range(BT):
            for q in range(4):
                post.append(
                    (
                        lambda x, j=j: x >= earliest(j),
                        False,
                        (
                            lambda j=j, q=q: e_transposes(j, q),
                            lambda j=j, q=q: (e_out(j, q), mark(("turned", j)) if q == 3 else None),
                            lambda j=j: j in e_sb,
                        ),
                    )
                )
                if q == 0 and 1 <= j <= last_phase:
                    post.append((lambda x, j=j: has_room(j - 1), True, (None, lambda j=j: e_quantise(j - 1, 0, NCH), None)))
                if q == 1 and j < last_phase:
                    post.append((lambda x: True, False, (None, lambda j=j: invert_sum(j), None)))
                if j == BT - 1 and q >= 1:
                    g1 = 2 * q + 2
                    if q == 2:
                        post.append((lambda x: True, False, (None, add_last_sums, None)))
                    post.append((lambda x: True, True, (None, lambda g1=g1: e_quantise(BT - 1, LAST_GROUPS[g1], g1), None)))
                    if q == 2:
                        post.append((lambda x: True, False, (None, lambda: invert_sum(BT - 1), None)))
                elif j >= last_phase and q == 3:
                    post.append((lambda x: True, False, (None, lambda j=j: invert_sum(j), None)))
                    post.append((lambda x, j=j: has_room(j), True, (None, lambda j=j: e_quantise(j, 0, NCH), None)))

        sums = [(j, 0, NCH) for j in range(BT - 1)] + [(BT - 1, g0, g1) for g1, g0 in LAST_GROUPS.items()]
        done = {"prep": 0, "post": 0, "codes": 0, "sums": 0, "outputs": 0}
        codes_at = {}

        def has_room(j):
            return j < done["outputs"] + CODE_BUFS

        def place_sum(x):
            j = done["outputs"]
            if j < OWN_FROM:
                if done["codes"] > j and done["prep"] == len(prep):
                    codes_at.setdefault(j, x)
                    if x >= codes_at[j] + SUM_LAG:
                        step(
                            lambda: (flush_mx(), finish(j)),
                            lambda: open_sum(j),
                            lambda: ("codes", j) in seen and "f" in seen,
                        )
                        done["outputs"] += 1
                        done["sums"] += 1
                return
            n = done["sums"]
            if n < len(sums) and n < done["codes"] and not (n == BT - 2 and done["post"] < len(post) - HOLD):
                step(lambda a=sums[n]: weighted_sum(*a))
                done["sums"] += 1
            elif n == len(sums) and done["post"] == len(post):
                step(lambda: finish(j))
                done["outputs"] += 1

        def place_piece(x):
            n = done["post"]
            if n < len(post) and post[n][0](x if x < BT * NCH + 1 else earliest(BT)):
                steps.append(post[n][2])
                done["post"] += 1
                done["codes"] += post[n][1]
            elif done["prep"] < len(prep):
                steps.append(prep[done["prep"]])
                done["prep"] += 1
            else:
                return False
            return True

        def key_step(c):
            step(
                lambda c=c: (
                    k_out(c),
                    [square_k(4 * c + s) for s in range(4)],
                ),
                lambda c=c: k_transposes(c),
            )
            if c == 0:
                step(lambda: t_out(0), lambda: t_transposes(0))

        for a, b in T_GROUPS:
            step(lambda a=a, b=b: norms_t(a, b))
        for c in range(3):
            key_step(c)
        for c in range(NCH):
            step(lambda c=c: whole_bank(c))
            if c == SQ_AT:
                step(lambda: (square_t(0), square_t(1)))
            if c + 3 < NCH:
                key_step(c + 3)
            if c == SQ_AT:
                step(lambda: scale_tt(nc.vector, 0, 2))
            if c >= 1:
                step(lambda c=c: (clamp_min(c - 1), mark(("bank", c - 1))))
        step(
            lambda: (
                [fold(8, s) for s in range(4)],
                [scores(x) for x in range(NCH, NCH + S_BANKS - 2)],
                clamp_min(7),
                mark(("bank", 7)),
                scores(NCH + S_BANKS - 2),
            )
        )

        def close_phase(a, b):
            step(lambda: (row_min(a, b), mark(("shift", b))))

        credit = 0
        for x in range(NCH, BT * NCH):
            i, c = x // NCH, x % NCH
            step(lambda x=x: (clamp_min(x), mark(("bank", x)), scores(x + S_BANKS - 1), mark(("scores", x + S_BANKS - 1))))
            if x in NORMS_AT:
                step(lambda ab=NORMS_AT[x]: scalar_norms(*ab))
            if c == 0 and i in phase_end:
                close_phase(phase_end[i], i)
            place_sum(x)
            credit = min(credit + (R0 if x < X1 else R1), POST_CAP)
            while credit >= 1 and place_piece(x):
                credit -= 1
        x = BT * NCH
        while done["outputs"] < BT:
            place_piece(x)
            if x == BT * NCH:
                close_phase(phase_end[BT], BT)
            place_sum(x)
            x += 1

        fed = [idx for idx in range(len(steps)) if steps[idx][0] is not None]
        state = {"next": 0, "open": 0}

        def feed(now):
            while state["next"] < len(fed) and state["open"] < X_BANKS and fed[state["next"]] - now <= LEAD:
                ahead, body, ready = steps[fed[state["next"]]]
                if ready is not None and not ready():
                    break
                ahead()
                state["next"] += 1
                state["open"] += 1

        warm_up(WARM_FIRST)
        feed(-1)
        for now in range(len(steps)):
            ahead, body, ready = steps[now]
            body()
            pump_act()
            if ahead is not None:
                state["open"] -= 1
            feed(now)
